import numpy as np
import ml_dtypes


def mxq(x, axis, fmt="e4m3"):
    dtype, down = {"e4m3": (ml_dtypes.float8_e4m3fn, 7), "e5m2": (ml_dtypes.float8_e5m2, 14)}[fmt]
    v = np.moveaxis(np.asarray(x, np.float32).astype(ml_dtypes.bfloat16).astype(np.float64), axis, -1)
    blocks = v.reshape(v.shape[:-1] + (-1, 32))
    amax = np.abs(blocks).max(-1, keepdims=True)
    byte = np.maximum(np.where(amax > 0, np.frexp(amax)[1] - 1 + 127, 0) - down, 1)
    scale = np.exp2(byte - 127.0)
    codes = (blocks / scale).astype(np.float32).astype(dtype).astype(np.float64)
    return np.moveaxis((codes * scale).reshape(v.shape), -1, axis)


WIDE = False


def mx_kscale(k):
    if not WIDE:
        return np.ones(k)
    levels = np.array([10, -10, 5, -5, 0])
    a = np.random.permutation(np.resize(levels, k // 512 * 4)).reshape(k // 512, 4)
    idx = np.arange(k)
    return np.exp2(a[idx // 512, idx % 128 // 32])


BF16 = ml_dtypes.bfloat16


def bf(x):
    return np.asarray(x, np.float32).astype(BF16)


def f64(x):
    return np.asarray(x).astype(np.float64)


E2M1 = np.array([0.0, 0.5, 1.0, 1.5, 2.0, 3.0, 4.0, 6.0, -0.0, -0.5, -1.0, -1.5, -2.0, -3.0, -4.0, -6.0])


def pack_weight(w, fmt):
    k, n = w.shape
    w = f64(bf(w)).reshape(k // 32, 32, n)
    amax = np.abs(w).max(1)
    if fmt == "e4m3":
        byte = np.frexp(amax)[1] - 1 + 127 - 7
    else:
        mant, ex = np.frexp(amax / 6.0)
        byte = np.where(mant > 0.5, ex, ex - 1) + 127
    byte = np.clip(np.where(amax > 0, byte, 1), 1, 254)
    scaled = (w * np.exp2(127.0 - byte)[:, None, :]).reshape(k, n).astype(np.float32)
    by_word = np.ascontiguousarray(scaled.reshape(k // 512, 128, 4, n).transpose(0, 1, 3, 2))
    if fmt == "e4m3":
        words = by_word.astype(ml_dtypes.float8_e4m3fn).view(np.uint8)
    else:
        c = by_word.astype(ml_dtypes.float4_e2m1fn).view(np.uint8) & 0xF
        words = c[..., 0::2] | (c[..., 1::2] << 4)
    return np.ascontiguousarray(words), np.ascontiguousarray(byte.astype(np.uint8).reshape(k // 512, 16, n))


def unpack_weight(words, scales, fmt):
    g, p, n, _ = words.shape
    if fmt == "e4m3":
        vals = np.ascontiguousarray(words).view(ml_dtypes.float8_e4m3fn).astype(np.float64)
    else:
        nib = np.empty((g, p, n, 4), np.uint8)
        nib[..., 0::2] = words & 0xF
        nib[..., 1::2] = words >> 4
        vals = E2M1[nib]
    vals = vals * np.repeat(np.exp2(scales.astype(np.float64) - 127.0), 8, axis=1)[..., None]
    return vals.transpose(0, 1, 3, 2).reshape(g * 512, n)


B, T, N, C, WIN, F = 2, 6, 512, 512, 3, 2
NW = T - WIN + 1


def sigmoid(v):
    return 1.0 / (1.0 + np.exp(-v))


def setup_inputs():
    t = mx_kscale(C)
    agg = bf(np.random.standard_normal((B, NW, N, C)) * t)
    stack = np.random.standard_normal((NW, F, C, 2 * C)) / np.sqrt(C) / t[:, None]
    words, scales = pack_weight(stack.reshape(-1, 2 * C), "e4m3")
    b = bf(np.random.standard_normal((NW, F, 2 * C)) * 0.3)
    return {"agg": agg, "W_words": words, "W_scales": scales, "b": b}


def reference(agg, W_words, W_scales, b):
    Wq = unpack_weight(W_words, W_scales, "e4m3").reshape(NW, F, C, 2 * C)
    pre = (mxq(f64(agg), 3, "e4m3")[:, :, None] @ Wq) + f64(b)[None, :, :, None, :]
    lhs, rhs = pre[..., :C], pre[..., C:]
    glu = lhs * sigmoid(rhs)
    return glu.max(axis=2)

@@ -1,0 +1,252 @@
+from contextlib import ExitStack
+
+import concourse.mybir as mybir
+from concourse.masks import make_identity
+
+F32 = mybir.dt.float32
+BF16 = mybir.dt.bfloat16
+I32 = mybir.dt.int32
+U32 = mybir.dt.uint32
+U8 = mybir.dt.uint8
+FP8X4 = mybir.dt.float8_e4m3fn_x4
+ALU = mybir.AluOpType
+ACT = mybir.ActivationFunctionType
+
+P = 128
+BATCH = 2
+WINDOWS = 4
+BRANCHES = 2
+NODES = 512
+CHANNELS = 512
+PAIRS = WINDOWS * BATCH
+NODE_TILES = NODES // P
+BLOCKS = CHANNELS // P
+ROUND_BLOCKS = 2
+ROUNDS_PER_PAIR = BLOCKS // ROUND_BLOCKS
+ROUNDS = PAIRS * ROUNDS_PER_PAIR
+HALF_NODES = NODES // 2
+HALVES = PAIRS * 2
+AHEAD = 3
+PLANES_PER_TILE = 4
+
+FLOPS = 2 * BATCH * WINDOWS * BRANCHES * NODES * CHANNELS * 2 * CHANNELS
+
+
+def tile_stsindividuallayer_pb_t_e_kernel(tc, agg, W_words, W_scales, b, out):
+    nc = tc.nc
+    with ExitStack() as ctx:
+        ctx.enter_context(tc.manual_schedule())
+        keep = ctx.enter_context(tc.tile_pool(name="keep", bufs=1))
+        gates = ctx.enter_context(tc.tile_pool(name="gates", bufs=6))
+        branches = ctx.enter_context(tc.tile_pool(name="branches", bufs=6))
+        mergeds = ctx.enter_context(tc.tile_pool(name="mergeds", bufs=4))
+        results = ctx.enter_context(tc.tile_pool(name="results", bufs=4))
+        acc_pool = ctx.enter_context(tc.psum_pool(name="acc", bufs=5))
+        flip_pool = ctx.enter_context(tc.psum_pool(name="flip", bufs=3))
+
+        x_raw = [keep.tile([P, NODE_TILES, CHANNELS], BF16, name="x_raw%d" % pair) for pair in range(PAIRS)]
+        grouped = [keep.tile([P, NODES * 4], BF16, name="grouped%d" % pair, align_bytes=64) for pair in range(PAIRS)]
+        x_codes = [keep.tile([P, NODES], U32, name="x_codes%d" % pair, align_bytes=64) for pair in range(PAIRS)]
+        x_scales = [keep.tile([P, NODES], U8, name="x_scales%d" % pair, align_bytes=64) for pair in range(PAIRS)]
+        matrices = WINDOWS * BRANCHES
+        w_codes = [keep.tile([P, 2 * CHANNELS], U32, name="w_codes%d" % e, align_bytes=64) for e in range(matrices)]
+        w_planes = [
+            keep.tile([P, 2 * CHANNELS], U8, name="w_planes%d" % s, align_bytes=64)
+            for s in range(matrices // PLANES_PER_TILE)
+        ]
+        ident = keep.tile([P, P], F32, name="ident")
+        b_rows = keep.tile([P, P], BF16, name="b_rows")
+        b_rows_f32 = keep.tile([P, P], F32, name="b_rows_f32")
+        bias_cols = matrices * 2 * BLOCKS
+        bias = keep.tile([P, bias_cols], F32, name="bias")
+        warm = keep.tile([P, 1], F32, name="warm")
+
+        for plane_tile in w_planes:
+            nc.vector.memset(plane_tile[:].bitcast(I32), 0)
+        nc.vector.memset(b_rows[:], 0.0)
+        nc.vector.memset(warm[:], 0.0)
+        make_identity(nc, ident[:])
+        nc.scalar.dma_start(out=b_rows[0:bias_cols, :], in_=b.rearrange("w f (c p) -> (w f c) p", p=P))
+        nc.scalar.activation(out=warm[:], in_=warm[:], func=ACT.Sigmoid)
+
+        def load_agg(pair):
+            w, i = divmod(pair, BATCH)
+            nc.sync.dma_start(out=x_raw[pair][:], in_=agg[i, w].rearrange("(p t) c -> p t c", t=NODE_TILES))
+
+        def load_weights(w):
+            for f in range(BRANCHES):
+                e = BRANCHES * w + f
+                nc.sync.dma_start(
+                    out=w_codes[e][:].bitcast(I32),
+                    in_=W_words[e].rearrange("p n t -> p (n t)").bitcast(I32),
+                )
+
+        def load_scale_planes():
+            for s in range(matrices // PLANES_PER_TILE):
+                for quadrant in range(4):
+                    nc.sync.dma_start(
+                        out=w_planes[s][32 * quadrant : 32 * quadrant + 16, :].bitcast(I32),
+                        in_=W_scales[
+                            PLANES_PER_TILE * s : PLANES_PER_TILE * (s + 1), 4 * quadrant : 4 * quadrant + 4, :
+                        ].bitcast(I32),
+                    )
+
+        load_agg(0)
+        load_scale_planes()
+        load_weights(0)
+        load_agg(1)
+        for w in range(1, WINDOWS):
+            load_agg(BATCH * w)
+            load_agg(BATCH * w + 1)
+            load_weights(w)
+
+        nc.vector.tensor_copy(out=b_rows_f32[:], in_=b_rows[:])
+        b_flip = flip_pool.tile([P, P], F32, tag="flip", name="b_flip")
+        nc.tensor.transpose(b_flip[:], b_rows_f32[:], ident[:])
+        nc.vector.tensor_copy(out=bias[:], in_=b_flip[:, 0:bias_cols])
+
+        agg_flips = {}
+
+        def transpose_agg_half(half):
+            pair, h = divmod(half, 2)
+            flipped = flip_pool.tile([P, 2, HALF_NODES], F32, tag="flip", name="agg_flip")
+            for a in range(HALF_NODES // P):
+                words = x_raw[pair][:, (HALF_NODES // P) * h + a, :].bitcast(F32)
+                for u in range(2):
+                    nc.tensor.transpose(flipped[:, u, P * a : P * (a + 1)], words[:, u : CHANNELS // 2 : 2], ident[:])
+            agg_flips[half] = flipped
+
+        def regroup_agg_half(half):
+            pair, h = divmod(half, 2)
+            words = grouped[pair][:].bitcast(F32)[:, 2 * HALF_NODES * h : 2 * HALF_NODES * (h + 1)]
+            nc.scalar.copy(
+                out=words.rearrange("p (c u) -> p c u", u=2),
+                in_=agg_flips[half][:].rearrange("p u c -> p c u"),
+            )
+
+        def quantise_agg_half(half):
+            pair, h = divmod(half, 2)
+            cols = slice(HALF_NODES * h, HALF_NODES * (h + 1))
+            nc.vector.quantize_mx(
+                out=x_codes[pair][:, cols].bitcast(FP8X4),
+                scales=x_scales[pair][:, cols],
+                in_=grouped[pair][:, 4 * HALF_NODES * h : 4 * HALF_NODES * (h + 1)],
+            )
+
+        def halves_of_round(r):
+            first = 2 if r == 0 else r + AHEAD
+            return range(first, min(r + AHEAD, HALVES - 1) + 1)
+
+        banks = {}
+        sigmoids = {}
+        merged = {}
+        out_flips = {}
+
+        def block_of(r, a):
+            return ROUND_BLOCKS * (r % ROUNDS_PER_PAIR) + a
+
+        def bias_col(r, a, f, part):
+            w = (r // ROUNDS_PER_PAIR) // BATCH
+            c = block_of(r, a) + (BLOCKS if part == "gate" else 0)
+            return (BRANCHES * w + f) * 2 * BLOCKS + c
+
+        def multiply(r):
+            pair = r // ROUNDS_PER_PAIR
+            w = pair // BATCH
+            for a in range(ROUND_BLOCKS):
+                for part in ("gate", "lin"):
+                    for f in range(BRANCHES):
+                        e = BRANCHES * w + f
+                        first_col = P * block_of(r, a) + (CHANNELS if part == "gate" else 0)
+                        cols = slice(first_col, first_col + P)
+                        offset = 4 * (e % PLANES_PER_TILE)
+                        bank = acc_pool.tile([P, NODES], F32, tag="acc", name="bank")
+                        nc.tensor.matmul_mx(
+                            out=bank[:],
+                            lhsT=w_codes[e][:, cols].bitcast(FP8X4),
+                            lhsT_scale=w_planes[e // PLANES_PER_TILE][offset:P, cols],
+                            rhs=x_codes[pair][:].bitcast(FP8X4),
+                            rhs_scale=x_scales[pair][:],
+                            start=True,
+                            stop=True,
+                        )
+                        banks[(r, a, f, part)] = bank
+
+        def open_gates(r):
+            for a in range(ROUND_BLOCKS):
+                for f in range(BRANCHES):
+                    col = bias_col(r, a, f, "gate")
+                    sig = gates.tile([P, NODES], F32, name="sig")
+                    nc.scalar.activation(
+                        out=sig[:], in_=banks[(r, a, f, "gate")][:], func=ACT.Sigmoid, bias=bias[:, col : col + 1], scale=1.0
+                    )
+                    sigmoids[(r, a, f)] = sig
+
+        def gated_branch(r, a, f):
+            col = bias_col(r, a, f, "lin")
+            glu = branches.tile([P, NODES], F32, name="glu")
+            nc.vector.scalar_tensor_tensor(
+                out=glu[:],
+                in0=banks[(r, a, f, "lin")][:],
+                scalar=bias[:, col : col + 1],
+                in1=sigmoids[(r, a, f)][:],
+                op0=ALU.add,
+                op1=ALU.mult,
+            )
+            return glu
+
+        def merge(r, a, glu_pair):
+            best = mergeds.tile([P, NODES], F32, name="best")
+            nc.vector.tensor_tensor(out=best[:], in0=glu_pair[0][:], in1=glu_pair[1][:], op=ALU.max)
+            merged[(r, a)] = best
+
+        def transpose_merged(r):
+            for a in range(ROUND_BLOCKS):
+                flipped = flip_pool.tile([P, NODE_TILES, P], F32, tag="flip", name="out_flip")
+                for t in range(NODE_TILES):
+                    nc.tensor.transpose(flipped[:, t, :], merged[(r, a)][:, P * t : P * (t + 1)], ident[:])
+                out_flips[(r, a)] = flipped
+
+        def store(r):
+            w, i = divmod(r // ROUNDS_PER_PAIR, BATCH)
+            width = ROUND_BLOCKS * P
+            result = results.tile([P, NODE_TILES, width], F32, name="result")
+            for a in range(ROUND_BLOCKS):
+                nc.scalar.copy(out=result[:, :, P * a : P * (a + 1)], in_=out_flips[(r, a)][:])
+            first_col = P * block_of(r, 0)
+            nc.sync.dma_start(
+                out=out[i, w].rearrange("(p t) c -> p t c", t=NODE_TILES)[:, :, first_col : first_col + width],
+                in_=result[:],
+            )
+
+        for half in range(2):
+            transpose_agg_half(half)
+            regroup_agg_half(half)
+        for half in range(2):
+            quantise_agg_half(half)
+
+        for r in range(ROUNDS + 1):
+            if r < ROUNDS:
+                multiply(r)
+            if r > 0:
+                transpose_merged(r - 1)
+            for half in halves_of_round(r):
+                transpose_agg_half(half)
+            if r < ROUNDS:
+                open_gates(r)
+            if r > 0:
+                store(r - 1)
+            for half in halves_of_round(r):
+                regroup_agg_half(half)
+            if r < ROUNDS:
+                glus = {}
+                for a in range(ROUND_BLOCKS):
+                    glus[(a, 0)] = gated_branch(r, a, 0)
+                    if a > 0:
+                        merge(r, a - 1, (glus[(a - 1, 0)], glus[(a - 1, 1)]))
+                    glus[(a, 1)] = gated_branch(r, a, 1)
+                if r > 0:
+                    for half in halves_of_round(r - 1):
+                        quantise_agg_half(half)
+                last = ROUND_BLOCKS - 1
+                merge(r, last, (glus[(last, 0)], glus[(last, 1)]))

@@ -41,8 +41,7 @@ def tile_stsindividuallayer_pb_t_e_kernel(tc, agg, W_words, W_scales, b, out):
         branches = ctx.enter_context(tc.tile_pool(name="branches", bufs=6))
         mergeds = ctx.enter_context(tc.tile_pool(name="mergeds", bufs=4))
         results = ctx.enter_context(tc.tile_pool(name="results", bufs=4))
-        acc_pool = ctx.enter_context(tc.psum_pool(name="acc", bufs=5))
-        flip_pool = ctx.enter_context(tc.psum_pool(name="flip", bufs=3))
+        psum = ctx.enter_context(tc.psum_pool(name="psum", bufs=8))
 
         x_raw = [keep.tile([P, NODE_TILES, CHANNELS], BF16, name="x_raw%d" % pair) for pair in range(PAIRS)]
         grouped = [keep.tile([P, NODES * 4], BF16, name="grouped%d" % pair, align_bytes=64) for pair in range(PAIRS)]
@@ -101,7 +100,7 @@ def tile_stsindividuallayer_pb_t_e_kernel(tc, agg, W_words, W_scales, b, out):
             load_weights(w)
 
         nc.vector.tensor_copy(out=b_rows_f32[:], in_=b_rows[:])
-        b_flip = flip_pool.tile([P, P], F32, tag="flip", name="b_flip")
+        b_flip = psum.tile([P, P], F32, tag="bank", name="b_flip")
         nc.tensor.transpose(b_flip[:], b_rows_f32[:], ident[:])
         nc.vector.tensor_copy(out=bias[:], in_=b_flip[:, 0:bias_cols])
 
@@ -109,7 +108,7 @@ def tile_stsindividuallayer_pb_t_e_kernel(tc, agg, W_words, W_scales, b, out):
 
         def transpose_agg_half(half):
             pair, h = divmod(half, 2)
-            flipped = flip_pool.tile([P, 2, HALF_NODES], F32, tag="flip", name="agg_flip")
+            flipped = psum.tile([P, 2, HALF_NODES], F32, tag="bank", name="agg_flip")
             for a in range(HALF_NODES // P):
                 words = x_raw[pair][:, (HALF_NODES // P) * h + a, :].bitcast(F32)
                 for u in range(2):
@@ -160,7 +159,7 @@ def tile_stsindividuallayer_pb_t_e_kernel(tc, agg, W_words, W_scales, b, out):
                         first_col = P * block_of(r, a) + (CHANNELS if part == "gate" else 0)
                         cols = slice(first_col, first_col + P)
                         offset = 4 * (e % PLANES_PER_TILE)
-                        bank = acc_pool.tile([P, NODES], F32, tag="acc", name="bank")
+                        bank = psum.tile([P, NODES], F32, tag="bank", name="bank")
                         nc.tensor.matmul_mx(
                             out=bank[:],
                             lhsT=w_codes[e][:, cols].bitcast(FP8X4),
@@ -202,7 +201,7 @@ def tile_stsindividuallayer_pb_t_e_kernel(tc, agg, W_words, W_scales, b, out):
 
         def transpose_merged(r):
             for a in range(ROUND_BLOCKS):
-                flipped = flip_pool.tile([P, NODE_TILES, P], F32, tag="flip", name="out_flip")
+                flipped = psum.tile([P, NODE_TILES, P], F32, tag="bank", name="out_flip")
                 for t in range(NODE_TILES):
                     nc.tensor.transpose(flipped[:, t, :], merged[(r, a)][:, P * t : P * (t + 1)], ident[:])
                 out_flips[(r, a)] = flipped
@@ -238,15 +237,10 @@ def tile_stsindividuallayer_pb_t_e_kernel(tc, agg, W_words, W_scales, b, out):
                 store(r - 1)
             for half in halves_of_round(r):
                 regroup_agg_half(half)
+            if r > 0:
+                for half in halves_of_round(r - 1):
+                    quantise_agg_half(half)
             if r < ROUNDS:
-                glus = {}
+                glus = [[gated_branch(r, a, f) for f in range(BRANCHES)] for a in range(ROUND_BLOCKS)]
                 for a in range(ROUND_BLOCKS):
-                    glus[(a, 0)] = gated_branch(r, a, 0)
-                    if a > 0:
-                        merge(r, a - 1, (glus[(a - 1, 0)], glus[(a - 1, 1)]))
-                    glus[(a, 1)] = gated_branch(r, a, 1)
-                if r > 0:
-                    for half in halves_of_round(r - 1):
-                        quantise_agg_half(half)
-                last = ROUND_BLOCKS - 1
-                merge(r, last, (glus[(last, 0)], glus[(last, 1)]))
+                    merge(r, a, glus[a])

@@ -40,10 +40,10 @@ def tile_stsindividuallayer_pb_t_e_kernel(tc, agg, W_words, W_scales, b, out):
         gates = ctx.enter_context(tc.tile_pool(name="gates", bufs=6))
         branches = ctx.enter_context(tc.tile_pool(name="branches", bufs=6))
         mergeds = ctx.enter_context(tc.tile_pool(name="mergeds", bufs=4))
-        results = ctx.enter_context(tc.tile_pool(name="results", bufs=4))
+        results = ctx.enter_context(tc.tile_pool(name="results", bufs=8))
         psum = ctx.enter_context(tc.psum_pool(name="psum", bufs=8))
 
-        x_raw = [keep.tile([P, NODE_TILES, CHANNELS], BF16, name="x_raw%d" % pair) for pair in range(PAIRS)]
+        x_raw = [keep.tile([P, HALF_NODES // P, CHANNELS], BF16, name="x_raw%d" % half) for half in range(HALVES)]
         grouped = [keep.tile([P, NODES * 4], BF16, name="grouped%d" % pair, align_bytes=64) for pair in range(PAIRS)]
         x_codes = [keep.tile([P, NODES], U32, name="x_codes%d" % pair, align_bytes=64) for pair in range(PAIRS)]
         x_scales = [keep.tile([P, NODES], U8, name="x_scales%d" % pair, align_bytes=64) for pair in range(PAIRS)]
@@ -70,7 +70,10 @@ def tile_stsindividuallayer_pb_t_e_kernel(tc, agg, W_words, W_scales, b, out):
 
         def load_agg(pair):
             w, i = divmod(pair, BATCH)
-            nc.sync.dma_start(out=x_raw[pair][:], in_=agg[i, w].rearrange("(p t) c -> p t c", t=NODE_TILES))
+            by_partition = agg[i, w].rearrange("(p t) c -> p t c", t=NODE_TILES)
+            tiles = HALF_NODES // P
+            for h in range(2):
+                nc.sync.dma_start(out=x_raw[2 * pair + h][:], in_=by_partition[:, tiles * h : tiles * (h + 1), :])
 
         def load_weights(w):
             for f in range(BRANCHES):
@@ -107,10 +110,9 @@ def tile_stsindividuallayer_pb_t_e_kernel(tc, agg, W_words, W_scales, b, out):
         agg_flips = {}
 
         def transpose_agg_half(half):
-            pair, h = divmod(half, 2)
             flipped = psum.tile([P, 2, HALF_NODES], F32, tag="bank", name="agg_flip")
             for a in range(HALF_NODES // P):
-                words = x_raw[pair][:, (HALF_NODES // P) * h + a, :].bitcast(F32)
+                words = x_raw[half][:, a, :].bitcast(F32)
                 for u in range(2):
                     nc.tensor.transpose(flipped[:, u, P * a : P * (a + 1)], words[:, u : CHANNELS // 2 : 2], ident[:])
             agg_flips[half] = flipped
@@ -208,15 +210,12 @@ def tile_stsindividuallayer_pb_t_e_kernel(tc, agg, W_words, W_scales, b, out):
 
         def store(r):
             w, i = divmod(r // ROUNDS_PER_PAIR, BATCH)
-            width = ROUND_BLOCKS * P
-            result = results.tile([P, NODE_TILES, width], F32, name="result")
+            by_partition = out[i, w].rearrange("(p t) c -> p t c", t=NODE_TILES)
             for a in range(ROUND_BLOCKS):
-                nc.scalar.copy(out=result[:, :, P * a : P * (a + 1)], in_=out_flips[(r, a)][:])
-            first_col = P * block_of(r, 0)
-            nc.sync.dma_start(
-                out=out[i, w].rearrange("(p t) c -> p t c", t=NODE_TILES)[:, :, first_col : first_col + width],
-                in_=result[:],
-            )
+                result = results.tile([P, NODE_TILES, P], F32, name="result")
+                nc.scalar.copy(out=result[:], in_=out_flips[(r, a)][:])
+                first_col = P * block_of(r, a)
+                nc.sync.dma_start(out=by_partition[:, :, first_col : first_col + P], in_=result[:])
 
         for half in range(2):
             transpose_agg_half(half)
@@ -241,6 +240,11 @@ def tile_stsindividuallayer_pb_t_e_kernel(tc, agg, W_words, W_scales, b, out):
                 for half in halves_of_round(r - 1):
                     quantise_agg_half(half)
             if r < ROUNDS:
-                glus = [[gated_branch(r, a, f) for f in range(BRANCHES)] for a in range(ROUND_BLOCKS)]
+                glus = {}
                 for a in range(ROUND_BLOCKS):
-                    merge(r, a, glus[a])
+                    glus[(a, 0)] = gated_branch(r, a, 0)
+                    if a > 0:
+                        merge(r, a - 1, (glus[(a - 1, 0)], glus[(a - 1, 1)]))
+                    glus[(a, 1)] = gated_branch(r, a, 1)
+                last = ROUND_BLOCKS - 1
+                merge(r, last, (glus[(last, 0)], glus[(last, 1)]))

@@ -240,11 +240,6 @@ def tile_stsindividuallayer_pb_t_e_kernel(tc, agg, W_words, W_scales, b, out):
                 for half in halves_of_round(r - 1):
                     quantise_agg_half(half)
             if r < ROUNDS:
-                glus = {}
+                glus = [[gated_branch(r, a, f) for f in range(BRANCHES)] for a in range(ROUND_BLOCKS)]
                 for a in range(ROUND_BLOCKS):
-                    glus[(a, 0)] = gated_branch(r, a, 0)
-                    if a > 0:
-                        merge(r, a - 1, (glus[(a - 1, 0)], glus[(a - 1, 1)]))
-                    glus[(a, 1)] = gated_branch(r, a, 1)
-                last = ROUND_BLOCKS - 1
-                merge(r, last, (glus[(last, 0)], glus[(last, 1)]))
+                    merge(r, a, glus[a])

@@ -24,9 +24,13 @@ BLOCKS = CHANNELS // P
 ROUND_BLOCKS = 2
 ROUNDS_PER_PAIR = BLOCKS // ROUND_BLOCKS
 ROUNDS = PAIRS * ROUNDS_PER_PAIR
+ROUND_COLS = ROUND_BLOCKS * P
 HALF_NODES = NODES // 2
 HALVES = PAIRS * 2
 AHEAD = 3
+SPIN_HEAD = 3
+SPIN_BEFORE_PASSES = 2
+HEAD_HALVES = 3
 PLANES_PER_TILE = 4
 
 FLOPS = 2 * BATCH * WINDOWS * BRANCHES * NODES * CHANNELS * 2 * CHANNELS
@@ -48,7 +52,10 @@ def tile_stsindividuallayer_pb_t_e_kernel(tc, agg, W_words, W_scales, b, out):
         x_codes = [keep.tile([P, NODES], U32, name="x_codes%d" % pair, align_bytes=64) for pair in range(PAIRS)]
         x_scales = [keep.tile([P, NODES], U8, name="x_scales%d" % pair, align_bytes=64) for pair in range(PAIRS)]
         matrices = WINDOWS * BRANCHES
-        w_codes = [keep.tile([P, 2 * CHANNELS], U32, name="w_codes%d" % e, align_bytes=64) for e in range(matrices)]
+        w_codes = [
+            [keep.tile([P, 2 * ROUND_COLS], U32, name="w_codes%d_%d" % (e, q), align_bytes=64) for q in range(ROUNDS_PER_PAIR)]
+            for e in range(matrices)
+        ]
         w_planes = [
             keep.tile([P, 2 * CHANNELS], U8, name="w_planes%d" % s, align_bytes=64)
             for s in range(matrices // PLANES_PER_TILE)
@@ -59,29 +66,37 @@ def tile_stsindividuallayer_pb_t_e_kernel(tc, agg, W_words, W_scales, b, out):
         bias_cols = matrices * 2 * BLOCKS
         bias = keep.tile([P, bias_cols], F32, name="bias")
         warm = keep.tile([P, 1], F32, name="warm")
+        spin_in = keep.tile([P, NODES], BF16, name="spin_in")
 
         for plane_tile in w_planes:
             nc.vector.memset(plane_tile[:].bitcast(I32), 0)
-        nc.vector.memset(b_rows[:], 0.0)
-        nc.vector.memset(warm[:], 0.0)
+        nc.vector.memset(b_rows[bias_cols:P, :], 0.0)
+        nc.gpsimd.memset(warm[:], 0.0)
+        nc.gpsimd.memset(spin_in[:], 0.0)
         make_identity(nc, ident[:])
         nc.scalar.dma_start(out=b_rows[0:bias_cols, :], in_=b.rearrange("w f (c p) -> (w f c) p", p=P))
         nc.scalar.activation(out=warm[:], in_=warm[:], func=ACT.Sigmoid)
 
-        def load_agg(pair):
+        def load_agg_half(half):
+            pair, h = divmod(half, 2)
             w, i = divmod(pair, BATCH)
             by_partition = agg[i, w].rearrange("(p t) c -> p t c", t=NODE_TILES)
             tiles = HALF_NODES // P
+            nc.sync.dma_start(out=x_raw[half][:], in_=by_partition[:, tiles * h : tiles * (h + 1), :])
+
+        def load_agg(pair):
             for h in range(2):
-                nc.sync.dma_start(out=x_raw[2 * pair + h][:], in_=by_partition[:, tiles * h : tiles * (h + 1), :])
+                load_agg_half(2 * pair + h)
 
         def load_weights(w):
-            for f in range(BRANCHES):
-                e = BRANCHES * w + f
-                nc.sync.dma_start(
-                    out=w_codes[e][:].bitcast(I32),
-                    in_=W_words[e].rearrange("p n t -> p (n t)").bitcast(I32),
-                )
+            for q in range(ROUNDS_PER_PAIR):
+                for f in range(BRANCHES):
+                    e = BRANCHES * w + f
+                    halves = W_words[e].rearrange("p n t -> p (n t)").bitcast(I32).rearrange("p (s c) -> p s c", s=2)
+                    nc.sync.dma_start(
+                        out=w_codes[e][q][:].bitcast(I32).rearrange("p (s c) -> p s c", s=2),
+                        in_=halves[:, :, ROUND_COLS * q : ROUND_COLS * (q + 1)],
+                    )
 
         def load_scale_planes():
             for s in range(matrices // PLANES_PER_TILE):
@@ -94,18 +109,22 @@ def tile_stsindividuallayer_pb_t_e_kernel(tc, agg, W_words, W_scales, b, out):
                     )
 
         load_agg(0)
+        load_agg_half(2)
         load_scale_planes()
         load_weights(0)
-        load_agg(1)
+        load_agg_half(3)
         for w in range(1, WINDOWS):
             load_agg(BATCH * w)
             load_agg(BATCH * w + 1)
             load_weights(w)
 
-        nc.vector.tensor_copy(out=b_rows_f32[:], in_=b_rows[:])
-        b_flip = psum.tile([P, P], F32, tag="bank", name="b_flip")
-        nc.tensor.transpose(b_flip[:], b_rows_f32[:], ident[:])
-        nc.vector.tensor_copy(out=bias[:], in_=b_flip[:, 0:bias_cols])
+
+        def spin(count):
+            spun = psum.tile([P, NODES], F32, tag="bank", name="spun")
+            for i in range(count):
+                nc.tensor.matmul(spun[:], lhsT=spin_in[:, 0:P], rhs=spin_in[:], start=True, stop=True)
+
+        spin(SPIN_HEAD)
 
         agg_flips = {}
 
@@ -135,8 +154,7 @@ def tile_stsindividuallayer_pb_t_e_kernel(tc, agg, W_words, W_scales, b, out):
             )
 
         def halves_of_round(r):
-            first = 2 if r == 0 else r + AHEAD
-            return range(first, min(r + AHEAD, HALVES - 1) + 1)
+            return range(r + AHEAD, min(r + AHEAD, HALVES - 1) + 1)
 
         banks = {}
         sigmoids = {}
@@ -160,11 +178,12 @@ def tile_stsindividuallayer_pb_t_e_kernel(tc, agg, W_words, W_scales, b, out):
                         e = BRANCHES * w + f
                         first_col = P * block_of(r, a) + (CHANNELS if part == "gate" else 0)
                         cols = slice(first_col, first_col + P)
+                        first_code = P * a + (ROUND_COLS if part == "gate" else 0)
                         offset = 4 * (e % PLANES_PER_TILE)
                         bank = psum.tile([P, NODES], F32, tag="bank", name="bank")
                         nc.tensor.matmul_mx(
                             out=bank[:],
-                            lhsT=w_codes[e][:, cols].bitcast(FP8X4),
+                            lhsT=w_codes[e][r % ROUNDS_PER_PAIR][:, first_code : first_code + P].bitcast(FP8X4),
                             lhsT_scale=w_planes[e // PLANES_PER_TILE][offset:P, cols],
                             rhs=x_codes[pair][:].bitcast(FP8X4),
                             rhs_scale=x_scales[pair][:],
@@ -220,7 +239,16 @@ def tile_stsindividuallayer_pb_t_e_kernel(tc, agg, W_words, W_scales, b, out):
         for half in range(2):
             transpose_agg_half(half)
             regroup_agg_half(half)
-        for half in range(2):
+        nc.vector.tensor_copy(out=b_rows_f32[:], in_=b_rows[:])
+        b_flip = psum.tile([P, P], F32, tag="bank", name="b_flip")
+        nc.tensor.transpose(b_flip[:], b_rows_f32[:], ident[:])
+        for half in range(2, HEAD_HALVES):
+            transpose_agg_half(half)
+            regroup_agg_half(half)
+        spin(SPIN_BEFORE_PASSES)
+        quantise_agg_half(0)
+        nc.vector.tensor_copy(out=bias[:], in_=b_flip[:, 0:bias_cols])
+        for half in range(1, HEAD_HALVES):
             quantise_agg_half(half)
 
         for r in range(ROUNDS + 1):

@@ -31,6 +31,7 @@ AHEAD = 3
 SPIN_HEAD = 3
 SPIN_BEFORE_PASSES = 2
 HEAD_HALVES = 3
+LAST_PIECES = 4
 PLANES_PER_TILE = 4
 
 FLOPS = 2 * BATCH * WINDOWS * BRANCHES * NODES * CHANNELS * 2 * CHANNELS
@@ -88,35 +89,36 @@ def tile_stsindividuallayer_pb_t_e_kernel(tc, agg, W_words, W_scales, b, out):
             for h in range(2):
                 load_agg_half(2 * pair + h)
 
-        def load_weights(w):
-            for q in range(ROUNDS_PER_PAIR):
-                for f in range(BRANCHES):
-                    e = BRANCHES * w + f
-                    halves = W_words[e].rearrange("p n t -> p (n t)").bitcast(I32).rearrange("p (s c) -> p s c", s=2)
-                    nc.sync.dma_start(
-                        out=w_codes[e][q][:].bitcast(I32).rearrange("p (s c) -> p s c", s=2),
-                        in_=halves[:, :, ROUND_COLS * q : ROUND_COLS * (q + 1)],
-                    )
+        def load_weights(w, q):
+            for f in range(BRANCHES):
+                e = BRANCHES * w + f
+                halves = W_words[e].rearrange("p n t -> p (n t)").bitcast(I32).rearrange("p (s c) -> p s c", s=2)
+                nc.sync.dma_start(
+                    out=w_codes[e][q][:].bitcast(I32).rearrange("p (s c) -> p s c", s=2),
+                    in_=halves[:, :, ROUND_COLS * q : ROUND_COLS * (q + 1)],
+                )
 
-        def load_scale_planes():
-            for s in range(matrices // PLANES_PER_TILE):
-                for quadrant in range(4):
-                    nc.sync.dma_start(
-                        out=w_planes[s][32 * quadrant : 32 * quadrant + 16, :].bitcast(I32),
-                        in_=W_scales[
-                            PLANES_PER_TILE * s : PLANES_PER_TILE * (s + 1), 4 * quadrant : 4 * quadrant + 4, :
-                        ].bitcast(I32),
-                    )
+        def load_scale_planes(s):
+            for quadrant in range(4):
+                nc.sync.dma_start(
+                    out=w_planes[s][32 * quadrant : 32 * quadrant + 16, :].bitcast(I32),
+                    in_=W_scales[
+                        PLANES_PER_TILE * s : PLANES_PER_TILE * (s + 1), 4 * quadrant : 4 * quadrant + 4, :
+                    ].bitcast(I32),
+                )
 
         load_agg(0)
         load_agg_half(2)
-        load_scale_planes()
-        load_weights(0)
+        load_scale_planes(0)
+        load_weights(0, 0)
+        load_weights(0, 1)
         load_agg_half(3)
+        load_scale_planes(1)
         for w in range(1, WINDOWS):
             load_agg(BATCH * w)
             load_agg(BATCH * w + 1)
-            load_weights(w)
+            for q in range(ROUNDS_PER_PAIR):
+                load_weights(w, q)
 
 
         def spin(count):
@@ -216,25 +218,37 @@ def tile_stsindividuallayer_pb_t_e_kernel(tc, agg, W_words, W_scales, b, out):
             return glu
 
         def merge(r, a, glu_pair):
-            best = mergeds.tile([P, NODES], F32, name="best")
-            nc.vector.tensor_tensor(out=best[:], in0=glu_pair[0][:], in1=glu_pair[1][:], op=ALU.max)
-            merged[(r, a)] = best
+            pieces = LAST_PIECES if (r, a) == (ROUNDS - 1, ROUND_BLOCKS - 1) else 1
+            width = NODES // pieces
+            merged[(r, a)] = []
+            for piece in range(pieces):
+                cols = slice(width * piece, width * (piece + 1))
+                best = mergeds.tile([P, width], F32, name="best")
+                nc.vector.tensor_tensor(out=best[:], in0=glu_pair[0][:, cols], in1=glu_pair[1][:, cols], op=ALU.max)
+                merged[(r, a)].append(best)
 
         def transpose_merged(r):
             for a in range(ROUND_BLOCKS):
-                flipped = psum.tile([P, NODE_TILES, P], F32, tag="bank", name="out_flip")
-                for t in range(NODE_TILES):
-                    nc.tensor.transpose(flipped[:, t, :], merged[(r, a)][:, P * t : P * (t + 1)], ident[:])
-                out_flips[(r, a)] = flipped
+                tiles = NODE_TILES // len(merged[(r, a)])
+                out_flips[(r, a)] = []
+                for best in merged[(r, a)]:
+                    flipped = psum.tile([P, tiles, P], F32, tag="bank", name="out_flip")
+                    for t in range(tiles):
+                        nc.tensor.transpose(flipped[:, t, :], best[:, P * t : P * (t + 1)], ident[:])
+                    out_flips[(r, a)].append(flipped)
 
         def store(r):
             w, i = divmod(r // ROUNDS_PER_PAIR, BATCH)
             by_partition = out[i, w].rearrange("(p t) c -> p t c", t=NODE_TILES)
             for a in range(ROUND_BLOCKS):
-                result = results.tile([P, NODE_TILES, P], F32, name="result")
-                nc.scalar.copy(out=result[:], in_=out_flips[(r, a)][:])
+                tiles = NODE_TILES // len(out_flips[(r, a)])
                 first_col = P * block_of(r, a)
-                nc.sync.dma_start(out=by_partition[:, :, first_col : first_col + P], in_=result[:])
+                for piece, flipped in enumerate(out_flips[(r, a)]):
+                    result = results.tile([P, tiles, P], F32, name="result")
+                    nc.scalar.copy(out=result[:], in_=flipped[:])
+                    nc.sync.dma_start(
+                        out=by_partition[:, tiles * piece : tiles * (piece + 1), first_col : first_col + P], in_=result[:]
+                    )
 
         for half in range(2):
             transpose_agg_half(half)
@@ -267,7 +281,10 @@ def tile_stsindividuallayer_pb_t_e_kernel(tc, agg, W_words, W_scales, b, out):
             if r > 0:
                 for half in halves_of_round(r - 1):
                     quantise_agg_half(half)
-            if r < ROUNDS:
+            if r < ROUNDS - 1:
                 glus = [[gated_branch(r, a, f) for f in range(BRANCHES)] for a in range(ROUND_BLOCKS)]
                 for a in range(ROUND_BLOCKS):
                     merge(r, a, glus[a])
+            elif r == ROUNDS - 1:
+                for a in range(ROUND_BLOCKS):
+                    merge(r, a, [gated_branch(r, a, f) for f in range(BRANCHES)])

@@ -32,6 +32,7 @@ SPIN_HEAD = 3
 SPIN_BEFORE_PASSES = 2
 HEAD_HALVES = 3
 LAST_PIECES = 4
+VECTOR_TILES = 1
 PLANES_PER_TILE = 4
 
 FLOPS = 2 * BATCH * WINDOWS * BRANCHES * NODES * CHANNELS * 2 * CHANNELS
@@ -237,18 +238,31 @@ def tile_stsindividuallayer_pb_t_e_kernel(tc, agg, W_words, W_scales, b, out):
                         nc.tensor.transpose(flipped[:, t, :], best[:, P * t : P * (t + 1)], ident[:])
                     out_flips[(r, a)].append(flipped)
 
-        def store(r):
+        shared_results = {}
+
+        def vector_share(r, a):
+            if len(out_flips[(r, a)]) == 1:
+                result = results.tile([P, NODE_TILES, P], F32, name="result")
+                first = NODE_TILES - VECTOR_TILES
+                nc.vector.tensor_copy(out=result[:, first:NODE_TILES, :], in_=out_flips[(r, a)][0][:, first:NODE_TILES, :])
+                shared_results[(r, a)] = result
+
+        def store(r, a):
             w, i = divmod(r // ROUNDS_PER_PAIR, BATCH)
             by_partition = out[i, w].rearrange("(p t) c -> p t c", t=NODE_TILES)
-            for a in range(ROUND_BLOCKS):
-                tiles = NODE_TILES // len(out_flips[(r, a)])
-                first_col = P * block_of(r, a)
-                for piece, flipped in enumerate(out_flips[(r, a)]):
+            tiles = NODE_TILES // len(out_flips[(r, a)])
+            first_col = P * block_of(r, a)
+            for piece, flipped in enumerate(out_flips[(r, a)]):
+                if (r, a) in shared_results:
+                    result = shared_results[(r, a)]
+                    mine = NODE_TILES - VECTOR_TILES
+                else:
                     result = results.tile([P, tiles, P], F32, name="result")
-                    nc.scalar.copy(out=result[:], in_=flipped[:])
-                    nc.sync.dma_start(
-                        out=by_partition[:, tiles * piece : tiles * (piece + 1), first_col : first_col + P], in_=result[:]
-                    )
+                    mine = tiles
+                nc.scalar.copy(out=result[:, 0:mine, :], in_=flipped[:, 0:mine, :])
+                nc.sync.dma_start(
+                    out=by_partition[:, tiles * piece : tiles * (piece + 1), first_col : first_col + P], in_=result[:]
+                )
 
         for half in range(2):
             transpose_agg_half(half)
@@ -275,16 +289,22 @@ def tile_stsindividuallayer_pb_t_e_kernel(tc, agg, W_words, W_scales, b, out):
             if r < ROUNDS:
                 open_gates(r)
             if r > 0:
-                store(r - 1)
-            for half in halves_of_round(r):
-                regroup_agg_half(half)
+                store(r - 1, 0)
             if r > 0:
                 for half in halves_of_round(r - 1):
                     quantise_agg_half(half)
-            if r < ROUNDS - 1:
-                glus = [[gated_branch(r, a, f) for f in range(BRANCHES)] for a in range(ROUND_BLOCKS)]
-                for a in range(ROUND_BLOCKS):
-                    merge(r, a, glus[a])
-            elif r == ROUNDS - 1:
-                for a in range(ROUND_BLOCKS):
-                    merge(r, a, [gated_branch(r, a, f) for f in range(BRANCHES)])
+            glus = {}
+            if r < ROUNDS:
+                glus[0] = [gated_branch(r, 0, f) for f in range(BRANCHES)]
+                if r == ROUNDS - 1:
+                    merge(r, 0, glus[0])
+            if r > 0:
+                vector_share(r - 1, 1)
+                store(r - 1, 1)
+            for half in halves_of_round(r):
+                regroup_agg_half(half)
+            if r < ROUNDS:
+                glus[1] = [gated_branch(r, 1, f) for f in range(BRANCHES)]
+                if r < ROUNDS - 1:
+                    merge(r, 0, glus[0])
+                merge(r, 1, glus[1])

@@ -33,6 +33,7 @@ SPIN_BEFORE_PASSES = 2
 HEAD_HALVES = 3
 LAST_PIECES = 4
 VECTOR_TILES = 1
+VECTOR_ROUNDS = ROUNDS // 2
 PLANES_PER_TILE = 4
 
 FLOPS = 2 * BATCH * WINDOWS * BRANCHES * NODES * CHANNELS * 2 * CHANNELS
@@ -241,7 +242,7 @@ def tile_stsindividuallayer_pb_t_e_kernel(tc, agg, W_words, W_scales, b, out):
         shared_results = {}
 
         def vector_share(r, a):
-            if len(out_flips[(r, a)]) == 1:
+            if len(out_flips[(r, a)]) == 1 and r < VECTOR_ROUNDS:
                 result = results.tile([P, NODE_TILES, P], F32, name="result")
                 first = NODE_TILES - VECTOR_TILES
                 nc.vector.tensor_copy(out=result[:, first:NODE_TILES, :], in_=out_flips[(r, a)][0][:, first:NODE_TILES, :])

@@ -28,8 +28,8 @@ ROUND_COLS = ROUND_BLOCKS * P
 HALF_NODES = NODES // 2
 HALVES = PAIRS * 2
 AHEAD = 3
-SPIN_HEAD = 3
-SPIN_BEFORE_PASSES = 2
+SPIN_HEAD = 5
+SPIN_BEFORE_PASSES = 3
 HEAD_HALVES = 3
 LAST_PIECES = 4
 VECTOR_TILES = 1

@@ -28,13 +28,14 @@ ROUND_COLS = ROUND_BLOCKS * P
 HALF_NODES = NODES // 2
 HALVES = PAIRS * 2
 AHEAD = 3
-SPIN_HEAD = 5
-SPIN_BEFORE_PASSES = 3
-HEAD_HALVES = 3
+SPIN_HEAD = 4
+SPIN_BEFORE_PASSES = 1
+SPLIT_BLOCKS = {(0, 0): (0, HALF_NODES, NODES)}
+FINE_HALVES = 2
+HEAD_HALVES = 2
 LAST_PIECES = 4
 VECTOR_TILES = 1
-VECTOR_ROUNDS = ROUNDS // 2
-PLANES_PER_TILE = 4
+VECTOR_ROUNDS = 6
 
 FLOPS = 2 * BATCH * WINDOWS * BRANCHES * NODES * CHANNELS * 2 * CHANNELS
 
@@ -56,13 +57,20 @@ def tile_stsindividuallayer_pb_t_e_kernel(tc, agg, W_words, W_scales, b, out):
         x_scales = [keep.tile([P, NODES], U8, name="x_scales%d" % pair, align_bytes=64) for pair in range(PAIRS)]
         matrices = WINDOWS * BRANCHES
         w_codes = [
-            [keep.tile([P, 2 * ROUND_COLS], U32, name="w_codes%d_%d" % (e, q), align_bytes=64) for q in range(ROUNDS_PER_PAIR)]
-            for e in range(matrices)
+            [
+                {
+                    part: [
+                        keep.tile([P, BRANCHES, width], U32, name="w_%s%d_%d_%d" % (part, w, q, x), align_bytes=64)
+                        for x in range(ROUND_COLS // width)
+                    ]
+                    for part in ("lin", "gate")
+                }
+                for q in range(ROUNDS_PER_PAIR)
+                for width in (P if (w, q) == (0, 0) else ROUND_COLS,)
+            ]
+            for w in range(WINDOWS)
         ]
-        w_planes = [
-            keep.tile([P, 2 * CHANNELS], U8, name="w_planes%d" % s, align_bytes=64)
-            for s in range(matrices // PLANES_PER_TILE)
-        ]
+        w_planes = [keep.tile([P, 2 * CHANNELS], U8, name="w_planes%d" % w, align_bytes=64) for w in range(WINDOWS)]
         ident = keep.tile([P, P], F32, name="ident")
         b_rows = keep.tile([P, P], BF16, name="b_rows")
         b_rows_f32 = keep.tile([P, P], F32, name="b_rows_f32")
@@ -92,36 +100,32 @@ def tile_stsindividuallayer_pb_t_e_kernel(tc, agg, W_words, W_scales, b, out):
                 load_agg_half(2 * pair + h)
 
         def load_weights(w, q):
-            for f in range(BRANCHES):
-                e = BRANCHES * w + f
-                halves = W_words[e].rearrange("p n t -> p (n t)").bitcast(I32).rearrange("p (s c) -> p s c", s=2)
-                nc.sync.dma_start(
-                    out=w_codes[e][q][:].bitcast(I32).rearrange("p (s c) -> p s c", s=2),
-                    in_=halves[:, :, ROUND_COLS * q : ROUND_COLS * (q + 1)],
-                )
+            words = W_words[BRANCHES * w : BRANCHES * (w + 1)].rearrange("f p n t -> p f (n t)").bitcast(I32)
+            for x in range(len(w_codes[w][q]["gate"])):
+                for part in ("gate", "lin"):
+                    codes = w_codes[w][q][part][x]
+                    width = ROUND_COLS // len(w_codes[w][q][part])
+                    first_col = ROUND_COLS * q + width * x + (CHANNELS if part == "gate" else 0)
+                    nc.sync.dma_start(out=codes[:].bitcast(I32), in_=words[:, :, first_col : first_col + width])
 
-        def load_scale_planes(s):
+        def load_scale_planes(w):
             for quadrant in range(4):
                 nc.sync.dma_start(
-                    out=w_planes[s][32 * quadrant : 32 * quadrant + 16, :].bitcast(I32),
-                    in_=W_scales[
-                        PLANES_PER_TILE * s : PLANES_PER_TILE * (s + 1), 4 * quadrant : 4 * quadrant + 4, :
-                    ].bitcast(I32),
+                    out=w_planes[w][32 * quadrant : 32 * quadrant + 4 * BRANCHES, :].bitcast(I32),
+                    in_=W_scales[BRANCHES * w : BRANCHES * (w + 1), 4 * quadrant : 4 * quadrant + 4, :].bitcast(I32),
                 )
 
         load_agg(0)
-        load_agg_half(2)
         load_scale_planes(0)
         load_weights(0, 0)
+        load_agg(1)
         load_weights(0, 1)
-        load_agg_half(3)
-        load_scale_planes(1)
         for w in range(1, WINDOWS):
             load_agg(BATCH * w)
+            load_scale_planes(w)
             load_agg(BATCH * w + 1)
             for q in range(ROUNDS_PER_PAIR):
                 load_weights(w, q)
-
 
         def spin(count):
             spun = psum.tile([P, NODES], F32, tag="bank", name="spun")
@@ -133,32 +137,43 @@ def tile_stsindividuallayer_pb_t_e_kernel(tc, agg, W_words, W_scales, b, out):
         agg_flips = {}
 
         def transpose_agg_half(half):
-            flipped = psum.tile([P, 2, HALF_NODES], F32, tag="bank", name="agg_flip")
-            for a in range(HALF_NODES // P):
-                words = x_raw[half][:, a, :].bitcast(F32)
-                for u in range(2):
-                    nc.tensor.transpose(flipped[:, u, P * a : P * (a + 1)], words[:, u : CHANNELS // 2 : 2], ident[:])
-            agg_flips[half] = flipped
+            tiles = HALF_NODES // P
+            per_bank = 1 if half < FINE_HALVES else tiles
+            agg_flips[half] = []
+            for first in range(0, tiles, per_bank):
+                flipped = psum.tile([P, 2, P * per_bank], F32, tag="bank", name="agg_flip")
+                for a in range(per_bank):
+                    words = x_raw[half][:, first + a, :].bitcast(F32)
+                    for u in range(2):
+                        nc.tensor.transpose(flipped[:, u, P * a : P * (a + 1)], words[:, u : CHANNELS // 2 : 2], ident[:])
+                agg_flips[half].append(flipped)
+
+        def agg_pieces(half):
+            pair, h = divmod(half, 2)
+            width = HALF_NODES // len(agg_flips[half])
+            first = HALF_NODES * h
+            return pair, [slice(c, c + width) for c in range(first, first + HALF_NODES, width)]
 
         def regroup_agg_half(half):
-            pair, h = divmod(half, 2)
-            words = grouped[pair][:].bitcast(F32)[:, 2 * HALF_NODES * h : 2 * HALF_NODES * (h + 1)]
-            nc.scalar.copy(
-                out=words.rearrange("p (c u) -> p c u", u=2),
-                in_=agg_flips[half][:].rearrange("p u c -> p c u"),
-            )
+            pair, pieces = agg_pieces(half)
+            for flipped, cols in zip(agg_flips[half], pieces):
+                words = grouped[pair][:].bitcast(F32)[:, 2 * cols.start : 2 * cols.stop]
+                nc.scalar.copy(
+                    out=words.rearrange("p (c u) -> p c u", u=2),
+                    in_=flipped[:].rearrange("p u c -> p c u"),
+                )
 
         def quantise_agg_half(half):
-            pair, h = divmod(half, 2)
-            cols = slice(HALF_NODES * h, HALF_NODES * (h + 1))
-            nc.vector.quantize_mx(
-                out=x_codes[pair][:, cols].bitcast(FP8X4),
-                scales=x_scales[pair][:, cols],
-                in_=grouped[pair][:, 4 * HALF_NODES * h : 4 * HALF_NODES * (h + 1)],
-            )
+            pair, pieces = agg_pieces(half)
+            for cols in pieces:
+                nc.vector.quantize_mx(
+                    out=x_codes[pair][:, cols].bitcast(FP8X4),
+                    scales=x_scales[pair][:, cols],
+                    in_=grouped[pair][:, 4 * cols.start : 4 * cols.stop],
+                )
 
         def halves_of_round(r):
-            return range(r + AHEAD, min(r + AHEAD, HALVES - 1) + 1)
+            return range(HEAD_HALVES if r == 0 else r + AHEAD, min(r + AHEAD, HALVES - 1) + 1)
 
         banks = {}
         sigmoids = {}
@@ -173,51 +188,63 @@ def tile_stsindividuallayer_pb_t_e_kernel(tc, agg, W_words, W_scales, b, out):
             c = block_of(r, a) + (BLOCKS if part == "gate" else 0)
             return (BRANCHES * w + f) * 2 * BLOCKS + c
 
+        def node_pieces(r, a):
+            bounds = SPLIT_BLOCKS.get((r, a), (0, NODES))
+            return [slice(lo, hi) for lo, hi in zip(bounds, bounds[1:])]
+
         def multiply(r):
-            pair = r // ROUNDS_PER_PAIR
+            pair, q = divmod(r, ROUNDS_PER_PAIR)
             w = pair // BATCH
             for a in range(ROUND_BLOCKS):
-                for part in ("gate", "lin"):
-                    for f in range(BRANCHES):
-                        e = BRANCHES * w + f
-                        first_col = P * block_of(r, a) + (CHANNELS if part == "gate" else 0)
-                        cols = slice(first_col, first_col + P)
-                        first_code = P * a + (ROUND_COLS if part == "gate" else 0)
-                        offset = 4 * (e % PLANES_PER_TILE)
-                        bank = psum.tile([P, NODES], F32, tag="bank", name="bank")
-                        nc.tensor.matmul_mx(
-                            out=bank[:],
-                            lhsT=w_codes[e][r % ROUNDS_PER_PAIR][:, first_code : first_code + P].bitcast(FP8X4),
-                            lhsT_scale=w_planes[e // PLANES_PER_TILE][offset:P, cols],
-                            rhs=x_codes[pair][:].bitcast(FP8X4),
-                            rhs_scale=x_scales[pair][:],
-                            start=True,
-                            stop=True,
-                        )
-                        banks[(r, a, f, part)] = bank
+                for nodes in node_pieces(r, a):
+                    for part in ("gate", "lin"):
+                        for f in range(BRANCHES):
+                            first_col = P * block_of(r, a) + (CHANNELS if part == "gate" else 0)
+                            width = ROUND_COLS // len(w_codes[w][q][part])
+                            x, first_code = divmod(P * a, width)
+                            bank = psum.tile([P, nodes.stop - nodes.start], F32, tag="bank", name="bank")
+                            nc.tensor.matmul_mx(
+                                out=bank[:],
+                                lhsT=w_codes[w][q][part][x][:, f, first_code : first_code + P].bitcast(FP8X4),
+                                lhsT_scale=w_planes[w][4 * f : P, first_col : first_col + P],
+                                rhs=x_codes[pair][:, nodes].bitcast(FP8X4),
+                                rhs_scale=x_scales[pair][:, nodes],
+                                start=True,
+                                stop=True,
+                            )
+                            banks.setdefault((r, a, f, part), []).append((bank, nodes))
 
         def open_gates(r):
             for a in range(ROUND_BLOCKS):
                 for f in range(BRANCHES):
-                    col = bias_col(r, a, f, "gate")
-                    sig = gates.tile([P, NODES], F32, name="sig")
-                    nc.scalar.activation(
-                        out=sig[:], in_=banks[(r, a, f, "gate")][:], func=ACT.Sigmoid, bias=bias[:, col : col + 1], scale=1.0
-                    )
-                    sigmoids[(r, a, f)] = sig
+                    sigmoids[(r, a, f)] = gates.tile([P, NODES], F32, name="sig")
+                for piece in range(len(node_pieces(r, a))):
+                    for f in range(BRANCHES):
+                        col = bias_col(r, a, f, "gate")
+                        bank, nodes = banks[(r, a, f, "gate")][piece]
+                        nc.scalar.activation(
+                            out=sigmoids[(r, a, f)][:, nodes],
+                            in_=bank[:],
+                            func=ACT.Sigmoid,
+                            bias=bias[:, col : col + 1],
+                            scale=1.0,
+                        )
 
-        def gated_branch(r, a, f):
-            col = bias_col(r, a, f, "lin")
-            glu = branches.tile([P, NODES], F32, name="glu")
-            nc.vector.scalar_tensor_tensor(
-                out=glu[:],
-                in0=banks[(r, a, f, "lin")][:],
-                scalar=bias[:, col : col + 1],
-                in1=sigmoids[(r, a, f)][:],
-                op0=ALU.add,
-                op1=ALU.mult,
-            )
-            return glu
+        def gated_branches(r, a):
+            glu_pair = [branches.tile([P, NODES], F32, name="glu") for f in range(BRANCHES)]
+            for piece in range(len(node_pieces(r, a))):
+                for f in range(BRANCHES):
+                    col = bias_col(r, a, f, "lin")
+                    bank, nodes = banks[(r, a, f, "lin")][piece]
+                    nc.vector.scalar_tensor_tensor(
+                        out=glu_pair[f][:, nodes],
+                        in0=bank[:],
+                        scalar=bias[:, col : col + 1],
+                        in1=sigmoids[(r, a, f)][:, nodes],
+                        op0=ALU.add,
+                        op1=ALU.mult,
+                    )
+            return glu_pair
 
         def merge(r, a, glu_pair):
             pieces = LAST_PIECES if (r, a) == (ROUNDS - 1, ROUND_BLOCKS - 1) else 1
@@ -283,6 +310,8 @@ def tile_stsindividuallayer_pb_t_e_kernel(tc, agg, W_words, W_scales, b, out):
         for r in range(ROUNDS + 1):
             if r < ROUNDS:
                 multiply(r)
+            if r == ROUNDS:
+                spin(5)
             if r > 0:
                 transpose_merged(r - 1)
             for half in halves_of_round(r):
@@ -296,7 +325,7 @@ def tile_stsindividuallayer_pb_t_e_kernel(tc, agg, W_words, W_scales, b, out):
                     quantise_agg_half(half)
             glus = {}
             if r < ROUNDS:
-                glus[0] = [gated_branch(r, 0, f) for f in range(BRANCHES)]
+                glus[0] = gated_branches(r, 0)
                 if r == ROUNDS - 1:
                     merge(r, 0, glus[0])
             if r > 0:
@@ -305,7 +334,7 @@ def tile_stsindividuallayer_pb_t_e_kernel(tc, agg, W_words, W_scales, b, out):
             for half in halves_of_round(r):
                 regroup_agg_half(half)
             if r < ROUNDS:
-                glus[1] = [gated_branch(r, 1, f) for f in range(BRANCHES)]
+                glus[1] = gated_branches(r, 1)
                 if r < ROUNDS - 1:
                     merge(r, 0, glus[0])
                 merge(r, 1, glus[1])

@@ -33,9 +33,10 @@ SPIN_BEFORE_PASSES = 1
 SPLIT_BLOCKS = {(0, 0): (0, HALF_NODES, NODES)}
 FINE_HALVES = 2
 HEAD_HALVES = 2
-LAST_PIECES = 4
+MERGE_LAG = 1
+LAST_PIECES = (2, 4)
 VECTOR_TILES = 1
-VECTOR_ROUNDS = 6
+VECTOR_ROUNDS = 7
 
 FLOPS = 2 * BATCH * WINDOWS * BRANCHES * NODES * CHANNELS * 2 * CHANNELS
 
@@ -176,6 +177,7 @@ def tile_stsindividuallayer_pb_t_e_kernel(tc, agg, W_words, W_scales, b, out):
             return range(HEAD_HALVES if r == 0 else r + AHEAD, min(r + AHEAD, HALVES - 1) + 1)
 
         banks = {}
+        glus = {}
         sigmoids = {}
         merged = {}
         out_flips = {}
@@ -214,47 +216,60 @@ def tile_stsindividuallayer_pb_t_e_kernel(tc, agg, W_words, W_scales, b, out):
                             )
                             banks.setdefault((r, a, f, part), []).append((bank, nodes))
 
-        def open_gates(r):
-            for a in range(ROUND_BLOCKS):
-                for f in range(BRANCHES):
-                    sigmoids[(r, a, f)] = gates.tile([P, NODES], F32, name="sig")
-                for piece in range(len(node_pieces(r, a))):
-                    for f in range(BRANCHES):
-                        col = bias_col(r, a, f, "gate")
-                        bank, nodes = banks[(r, a, f, "gate")][piece]
-                        nc.scalar.activation(
-                            out=sigmoids[(r, a, f)][:, nodes],
-                            in_=bank[:],
-                            func=ACT.Sigmoid,
-                            bias=bias[:, col : col + 1],
-                            scale=1.0,
-                        )
-
-        def gated_branches(r, a):
-            glu_pair = [branches.tile([P, NODES], F32, name="glu") for f in range(BRANCHES)]
+        def open_gates(r, a):
+            for f in range(BRANCHES):
+                sigmoids[(r, a, f)] = gates.tile([P, NODES], F32, name="sig")
             for piece in range(len(node_pieces(r, a))):
                 for f in range(BRANCHES):
-                    col = bias_col(r, a, f, "lin")
-                    bank, nodes = banks[(r, a, f, "lin")][piece]
-                    nc.vector.scalar_tensor_tensor(
-                        out=glu_pair[f][:, nodes],
-                        in0=bank[:],
-                        scalar=bias[:, col : col + 1],
-                        in1=sigmoids[(r, a, f)][:, nodes],
-                        op0=ALU.add,
-                        op1=ALU.mult,
+                    col = bias_col(r, a, f, "gate")
+                    bank, nodes = banks[(r, a, f, "gate")][piece]
+                    nc.scalar.activation(
+                        out=sigmoids[(r, a, f)][:, nodes],
+                        in_=bank[:],
+                        func=ACT.Sigmoid,
+                        bias=bias[:, col : col + 1],
+                        scale=1.0,
                     )
-            return glu_pair
 
-        def merge(r, a, glu_pair):
-            pieces = LAST_PIECES if (r, a) == (ROUNDS - 1, ROUND_BLOCKS - 1) else 1
+        def gated_branch(r, a, f, piece, part=slice(None)):
+            if (r, a, f) not in glus:
+                glus[(r, a, f)] = branches.tile([P, NODES], F32, name="glu")
+            col = bias_col(r, a, f, "lin")
+            bank, nodes = banks[(r, a, f, "lin")][piece]
+            nc.vector.scalar_tensor_tensor(
+                out=glus[(r, a, f)][:, nodes][:, part],
+                in0=bank[:, part],
+                scalar=bias[:, col : col + 1],
+                in1=sigmoids[(r, a, f)][:, nodes][:, part],
+                op0=ALU.add,
+                op1=ALU.mult,
+            )
+
+        def gated_branches(r, a):
+            for piece in range(len(node_pieces(r, a))):
+                for f in range(BRANCHES):
+                    gated_branch(r, a, f, piece)
+
+        def maximum(r, a, out, cols):
+            nc.vector.tensor_tensor(out=out, in0=glus[(r, a, 0)][:, cols], in1=glus[(r, a, 1)][:, cols], op=ALU.max)
+
+        def merge(r, a, cols=slice(0, NODES)):
+            if (r, a) not in merged:
+                merged[(r, a)] = [mergeds.tile([P, NODES], F32, name="best")]
+            maximum(r, a, merged[(r, a)][0][:, cols], cols)
+
+        def gate_and_merge(r, a, pieces):
+            gated_branch(r, a, 0, 0)
             width = NODES // pieces
+            cols = [slice(width * piece, width * (piece + 1)) for piece in range(pieces)]
             merged[(r, a)] = []
-            for piece in range(pieces):
-                cols = slice(width * piece, width * (piece + 1))
-                best = mergeds.tile([P, width], F32, name="best")
-                nc.vector.tensor_tensor(out=best[:], in0=glu_pair[0][:, cols], in1=glu_pair[1][:, cols], op=ALU.max)
-                merged[(r, a)].append(best)
+            for piece in range(pieces + MERGE_LAG):
+                if piece < pieces:
+                    gated_branch(r, a, 1, 0, cols[piece])
+                if piece >= MERGE_LAG:
+                    best = mergeds.tile([P, width], F32, name="best")
+                    maximum(r, a, best[:], cols[piece - MERGE_LAG])
+                    merged[(r, a)].append(best)
 
         def transpose_merged(r):
             for a in range(ROUND_BLOCKS):
@@ -311,30 +326,33 @@ def tile_stsindividuallayer_pb_t_e_kernel(tc, agg, W_words, W_scales, b, out):
             if r < ROUNDS:
                 multiply(r)
             if r == ROUNDS:
-                spin(5)
+                spin(4)
             if r > 0:
                 transpose_merged(r - 1)
             for half in halves_of_round(r):
                 transpose_agg_half(half)
             if r < ROUNDS:
-                open_gates(r)
+                open_gates(r, 0)
+                open_gates(r, 1)
             if r > 0:
                 store(r - 1, 0)
             if r > 0:
                 for half in halves_of_round(r - 1):
                     quantise_agg_half(half)
-            glus = {}
-            if r < ROUNDS:
-                glus[0] = gated_branches(r, 0)
-                if r == ROUNDS - 1:
-                    merge(r, 0, glus[0])
+            if r < ROUNDS - 1:
+                gated_branches(r, 0)
+            elif r == ROUNDS - 1:
+                gate_and_merge(r, 0, LAST_PIECES[0])
+            if r == 0:
+                merge(r, 0, slice(0, HALF_NODES))
             if r > 0:
                 vector_share(r - 1, 1)
                 store(r - 1, 1)
             for half in halves_of_round(r):
                 regroup_agg_half(half)
-            if r < ROUNDS:
-                glus[1] = gated_branches(r, 1)
-                if r < ROUNDS - 1:
-                    merge(r, 0, glus[0])
-                merge(r, 1, glus[1])
+            if r < ROUNDS - 1:
+                gated_branches(r, 1)
+                merge(r, 0, slice(HALF_NODES if r == 0 else 0, NODES))
+                merge(r, 1)
+            elif r == ROUNDS - 1:
+                gate_and_merge(r, 1, LAST_PIECES[1])

@@ -53,15 +53,15 @@ def tile_stsindividuallayer_pb_t_e_kernel(tc, agg, W_words, W_scales, b, out):
         psum = ctx.enter_context(tc.psum_pool(name="psum", bufs=8))
 
         x_raw = [keep.tile([P, HALF_NODES // P, CHANNELS], BF16, name="x_raw%d" % half) for half in range(HALVES)]
-        grouped = [keep.tile([P, NODES * 4], BF16, name="grouped%d" % pair, align_bytes=64) for pair in range(PAIRS)]
-        x_codes = [keep.tile([P, NODES], U32, name="x_codes%d" % pair, align_bytes=64) for pair in range(PAIRS)]
-        x_scales = [keep.tile([P, NODES], U8, name="x_scales%d" % pair, align_bytes=64) for pair in range(PAIRS)]
+        grouped = [keep.tile([P, NODES * 4], BF16, name="grouped%d" % pair, align_bytes=256) for pair in range(PAIRS)]
+        x_codes = [keep.tile([P, NODES], U32, name="x_codes%d" % pair, align_bytes=256) for pair in range(PAIRS)]
+        x_scales = [keep.tile([P, NODES], U8, name="x_scales%d" % pair, align_bytes=256) for pair in range(PAIRS)]
         matrices = WINDOWS * BRANCHES
         w_codes = [
             [
                 {
                     part: [
-                        keep.tile([P, BRANCHES, width], U32, name="w_%s%d_%d_%d" % (part, w, q, x), align_bytes=64)
+                        keep.tile([P, BRANCHES, width], U32, name="w_%s%d_%d_%d" % (part, w, q, x), align_bytes=256)
                         for x in range(ROUND_COLS // width)
                     ]
                     for part in ("lin", "gate")
@@ -71,7 +71,7 @@ def tile_stsindividuallayer_pb_t_e_kernel(tc, agg, W_words, W_scales, b, out):
             ]
             for w in range(WINDOWS)
         ]
-        w_planes = [keep.tile([P, 2 * CHANNELS], U8, name="w_planes%d" % w, align_bytes=64) for w in range(WINDOWS)]
+        w_planes = [keep.tile([P, 2 * CHANNELS], U8, name="w_planes%d" % w, align_bytes=256) for w in range(WINDOWS)]
         ident = keep.tile([P, P], F32, name="ident")
         b_rows = keep.tile([P, P], BF16, name="b_rows")
         b_rows_f32 = keep.tile([P, P], F32, name="b_rows_f32")

@@ -33,10 +33,13 @@ SPIN_BEFORE_PASSES = 1
 SPLIT_BLOCKS = {(0, 0): (0, HALF_NODES, NODES)}
 FINE_HALVES = 2
 HEAD_HALVES = 2
+POOL_ROUNDS = (1, 3, 5, 7, 9, 11)
+POOL_LAG = 2
+POOL_COLS = 384
 MERGE_LAG = 1
 LAST_PIECES = (2, 4)
 VECTOR_TILES = 1
-VECTOR_ROUNDS = 7
+VECTOR_ROUNDS = 12
 
 FLOPS = 2 * BATCH * WINDOWS * BRANCHES * NODES * CHANNELS * 2 * CHANNELS
 
@@ -47,8 +50,8 @@ def tile_stsindividuallayer_pb_t_e_kernel(tc, agg, W_words, W_scales, b, out):
         ctx.enter_context(tc.manual_schedule())
         keep = ctx.enter_context(tc.tile_pool(name="keep", bufs=1))
         gates = ctx.enter_context(tc.tile_pool(name="gates", bufs=6))
-        branches = ctx.enter_context(tc.tile_pool(name="branches", bufs=6))
-        mergeds = ctx.enter_context(tc.tile_pool(name="mergeds", bufs=4))
+        branches = ctx.enter_context(tc.tile_pool(name="branches", bufs=14))
+        mergeds = ctx.enter_context(tc.tile_pool(name="mergeds", bufs=8))
         results = ctx.enter_context(tc.tile_pool(name="results", bufs=8))
         psum = ctx.enter_context(tc.psum_pool(name="psum", bufs=8))
 
@@ -271,8 +274,41 @@ def tile_stsindividuallayer_pb_t_e_kernel(tc, agg, W_words, W_scales, b, out):
                     maximum(r, a, best[:], cols[piece - MERGE_LAG])
                     merged[(r, a)].append(best)
 
-        def transpose_merged(r):
-            for a in range(ROUND_BLOCKS):
+        def half_words(half):
+            pair, h = divmod(half, 2)
+            return grouped[pair][:].bitcast(F32)[:, 2 * HALF_NODES * h : 2 * HALF_NODES * (h + 1)]
+
+        pool_parts = (slice(0, POOL_COLS // 2), slice(POOL_COLS // 2, POOL_COLS))
+
+        def pool_start(r):
+            diff = half_words(r + AHEAD)
+            nc.gpsimd.tensor_tensor(
+                out=diff[:, 0:POOL_COLS], in0=glus[(r, 1, 1)][:, 0:POOL_COLS], in1=glus[(r, 1, 0)][:, 0:POOL_COLS], op=ALU.subtract
+            )
+            nc.gpsimd.tensor_scalar(
+                out=diff[:, pool_parts[0]], in0=diff[:, pool_parts[0]], scalar1=0.0, scalar2=None, op0=ALU.max
+            )
+
+        def pool_finish(r):
+            diff = half_words(r + AHEAD)
+            rest = half_words(r + AHEAD + 1)
+            width = POOL_COLS // 2
+            nc.gpsimd.tensor_scalar(out=rest[:, 0:width], in0=diff[:, pool_parts[1]], scalar1=0.0, scalar2=None, op0=ALU.max)
+            for part, gain in zip(pool_parts, (diff[:, pool_parts[0]], rest[:, 0:width])):
+                nc.gpsimd.tensor_tensor(out=merged[(r, 1)][0][:, part], in0=glus[(r, 1, 0)][:, part], in1=gain, op=ALU.add)
+
+        def due(r):
+            blocks = []
+            if r > 0:
+                blocks.append((r - 1, 0))
+                if r - 1 not in POOL_ROUNDS:
+                    blocks.append((r - 1, 1))
+            if r - 1 - POOL_LAG in POOL_ROUNDS:
+                blocks.append((r - 1 - POOL_LAG, 1))
+            return blocks
+
+        def transpose_merged(blocks):
+            for r, a in blocks:
                 tiles = NODE_TILES // len(merged[(r, a)])
                 out_flips[(r, a)] = []
                 for best in merged[(r, a)]:
@@ -327,8 +363,7 @@ def tile_stsindividuallayer_pb_t_e_kernel(tc, agg, W_words, W_scales, b, out):
                 multiply(r)
             if r == ROUNDS:
                 spin(4)
-            if r > 0:
-                transpose_merged(r - 1)
+            transpose_merged(due(r))
             for half in halves_of_round(r):
                 transpose_agg_half(half)
             if r < ROUNDS:
@@ -345,14 +380,18 @@ def tile_stsindividuallayer_pb_t_e_kernel(tc, agg, W_words, W_scales, b, out):
                 gate_and_merge(r, 0, LAST_PIECES[0])
             if r == 0:
                 merge(r, 0, slice(0, HALF_NODES))
-            if r > 0:
-                vector_share(r - 1, 1)
-                store(r - 1, 1)
+            for block in due(r)[1:]:
+                vector_share(*block)
+                store(*block)
+            if r - 1 in POOL_ROUNDS:
+                pool_start(r - 1)
+            if r - 2 in POOL_ROUNDS:
+                pool_finish(r - 2)
             for half in halves_of_round(r):
                 regroup_agg_half(half)
             if r < ROUNDS - 1:
                 gated_branches(r, 1)
                 merge(r, 0, slice(HALF_NODES if r == 0 else 0, NODES))
-                merge(r, 1)
+                merge(r, 1, slice(POOL_COLS if r in POOL_ROUNDS else 0, NODES))
             elif r == ROUNDS - 1:
                 gate_and_merge(r, 1, LAST_PIECES[1])

@@ -35,11 +35,11 @@ FINE_HALVES = 2
 HEAD_HALVES = 2
 POOL_ROUNDS = (1, 3, 5, 7, 9, 11)
 POOL_LAG = 2
-POOL_COLS = 384
+POOL_COLS = 320
 MERGE_LAG = 1
 LAST_PIECES = (2, 4)
-VECTOR_TILES = 1
-VECTOR_ROUNDS = 12
+VECTOR_SET = (2, 4, 8, 10)
+VPOS = 2
 
 FLOPS = 2 * BATCH * WINDOWS * BRANCHES * NODES * CHANNELS * 2 * CHANNELS
 
@@ -317,31 +317,22 @@ def tile_stsindividuallayer_pb_t_e_kernel(tc, agg, W_words, W_scales, b, out):
                         nc.tensor.transpose(flipped[:, t, :], best[:, P * t : P * (t + 1)], ident[:])
                     out_flips[(r, a)].append(flipped)
 
-        shared_results = {}
-
-        def vector_share(r, a):
-            if len(out_flips[(r, a)]) == 1 and r < VECTOR_ROUNDS:
-                result = results.tile([P, NODE_TILES, P], F32, name="result")
-                first = NODE_TILES - VECTOR_TILES
-                nc.vector.tensor_copy(out=result[:, first:NODE_TILES, :], in_=out_flips[(r, a)][0][:, first:NODE_TILES, :])
-                shared_results[(r, a)] = result
-
-        def store(r, a):
+        def store(r, a, copy=None):
             w, i = divmod(r // ROUNDS_PER_PAIR, BATCH)
             by_partition = out[i, w].rearrange("(p t) c -> p t c", t=NODE_TILES)
             tiles = NODE_TILES // len(out_flips[(r, a)])
             first_col = P * block_of(r, a)
             for piece, flipped in enumerate(out_flips[(r, a)]):
-                if (r, a) in shared_results:
-                    result = shared_results[(r, a)]
-                    mine = NODE_TILES - VECTOR_TILES
-                else:
-                    result = results.tile([P, tiles, P], F32, name="result")
-                    mine = tiles
-                nc.scalar.copy(out=result[:, 0:mine, :], in_=flipped[:, 0:mine, :])
+                result = results.tile([P, tiles, P], F32, name="result")
+                (copy or nc.scalar.copy)(out=result[:], in_=flipped[:])
                 nc.sync.dma_start(
                     out=by_partition[:, tiles * piece : tiles * (piece + 1), first_col : first_col + P], in_=result[:]
                 )
+
+        def vector_store(r, pos):
+            for block in due(r)[1:]:
+                if block[0] in VECTOR_SET and pos == VPOS:
+                    store(*block, copy=nc.vector.tensor_copy)
 
         for half in range(2):
             transpose_agg_half(half)
@@ -381,8 +372,9 @@ def tile_stsindividuallayer_pb_t_e_kernel(tc, agg, W_words, W_scales, b, out):
             if r == 0:
                 merge(r, 0, slice(0, HALF_NODES))
             for block in due(r)[1:]:
-                vector_share(*block)
-                store(*block)
+                if block[0] not in VECTOR_SET:
+                    store(*block)
+            vector_store(r, 0)
             if r - 1 in POOL_ROUNDS:
                 pool_start(r - 1)
             if r - 2 in POOL_ROUNDS:
@@ -390,8 +382,15 @@ def tile_stsindividuallayer_pb_t_e_kernel(tc, agg, W_words, W_scales, b, out):
             for half in halves_of_round(r):
                 regroup_agg_half(half)
             if r < ROUNDS - 1:
-                gated_branches(r, 1)
+                if r == 0:
+                    gated_branches(r, 1)
+                else:
+                    gated_branch(r, 1, 0, 0)
+                    vector_store(r, 1)
+                    gated_branch(r, 1, 1, 0)
+                    vector_store(r, 2)
                 merge(r, 0, slice(HALF_NODES if r == 0 else 0, NODES))
                 merge(r, 1, slice(POOL_COLS if r in POOL_ROUNDS else 0, NODES))
+                vector_store(r, 3)
             elif r == ROUNDS - 1:
                 gate_and_merge(r, 1, LAST_PIECES[1])

@@ -21,25 +21,23 @@ CHANNELS = 512
 PAIRS = WINDOWS * BATCH
 NODE_TILES = NODES // P
 BLOCKS = CHANNELS // P
-ROUND_BLOCKS = 2
-ROUNDS_PER_PAIR = BLOCKS // ROUND_BLOCKS
-ROUNDS = PAIRS * ROUNDS_PER_PAIR
-ROUND_COLS = ROUND_BLOCKS * P
 HALF_NODES = NODES // 2
 HALVES = PAIRS * 2
-AHEAD = 3
+SHORT_PAIRS = (0, 6, 7)
+VECTOR_SET = (4, 5, 6)
+POOL_PAIRS = (1, 2, 3, 4)
+POOL_COLS = 448
+LATE_MERGE = 1
 SPIN_HEAD = 4
 SPIN_BEFORE_PASSES = 1
-SPLIT_BLOCKS = {(0, 0): (0, HALF_NODES, NODES)}
+SPIN_TAIL = 4
 FINE_HALVES = 2
-HEAD_HALVES = 2
-POOL_ROUNDS = (1, 3, 5, 7, 9, 11)
-POOL_LAG = 2
-POOL_COLS = 320
-MERGE_LAG = 1
 LAST_PIECES = (2, 4)
-VECTOR_SET = (2, 4, 8, 10)
-VPOS = 2
+MERGE_LAG = 1
+GATES = 10
+BRANCH_BUFS = 12
+MERGED = 8
+RESULTS = 8
 
 FLOPS = 2 * BATCH * WINDOWS * BRANCHES * NODES * CHANNELS * 2 * CHANNELS
 
@@ -49,36 +47,32 @@ def tile_stsindividuallayer_pb_t_e_kernel(tc, agg, W_words, W_scales, b, out):
     with ExitStack() as ctx:
         ctx.enter_context(tc.manual_schedule())
         keep = ctx.enter_context(tc.tile_pool(name="keep", bufs=1))
-        gates = ctx.enter_context(tc.tile_pool(name="gates", bufs=6))
-        branches = ctx.enter_context(tc.tile_pool(name="branches", bufs=14))
-        mergeds = ctx.enter_context(tc.tile_pool(name="mergeds", bufs=8))
-        results = ctx.enter_context(tc.tile_pool(name="results", bufs=8))
+        gates = ctx.enter_context(tc.tile_pool(name="gates", bufs=GATES))
+        branches = ctx.enter_context(tc.tile_pool(name="branches", bufs=BRANCH_BUFS))
+        mergeds = ctx.enter_context(tc.tile_pool(name="mergeds", bufs=MERGED))
+        results = ctx.enter_context(tc.tile_pool(name="results", bufs=RESULTS))
         psum = ctx.enter_context(tc.psum_pool(name="psum", bufs=8))
 
         x_raw = [keep.tile([P, HALF_NODES // P, CHANNELS], BF16, name="x_raw%d" % half) for half in range(HALVES)]
         grouped = [keep.tile([P, NODES * 4], BF16, name="grouped%d" % pair, align_bytes=256) for pair in range(PAIRS)]
         x_codes = [keep.tile([P, NODES], U32, name="x_codes%d" % pair, align_bytes=256) for pair in range(PAIRS)]
         x_scales = [keep.tile([P, NODES], U8, name="x_scales%d" % pair, align_bytes=256) for pair in range(PAIRS)]
-        matrices = WINDOWS * BRANCHES
         w_codes = [
-            [
-                {
-                    part: [
-                        keep.tile([P, BRANCHES, width], U32, name="w_%s%d_%d_%d" % (part, w, q, x), align_bytes=256)
-                        for x in range(ROUND_COLS // width)
-                    ]
-                    for part in ("lin", "gate")
-                }
-                for q in range(ROUNDS_PER_PAIR)
-                for width in (P if (w, q) == (0, 0) else ROUND_COLS,)
-            ]
+            {
+                part: [
+                    keep.tile([P, BRANCHES, width], U32, name="w_%s%d_%d" % (part, w, x), align_bytes=256)
+                    for x in range(CHANNELS // width)
+                ]
+                for part in ("lin", "gate")
+            }
             for w in range(WINDOWS)
+            for width in (P if w == 0 else 2 * P,)
         ]
         w_planes = [keep.tile([P, 2 * CHANNELS], U8, name="w_planes%d" % w, align_bytes=256) for w in range(WINDOWS)]
         ident = keep.tile([P, P], F32, name="ident")
         b_rows = keep.tile([P, P], BF16, name="b_rows")
         b_rows_f32 = keep.tile([P, P], F32, name="b_rows_f32")
-        bias_cols = matrices * 2 * BLOCKS
+        bias_cols = WINDOWS * BRANCHES * 2 * BLOCKS
         bias = keep.tile([P, bias_cols], F32, name="bias")
         warm = keep.tile([P, 1], F32, name="warm")
         spin_in = keep.tile([P, NODES], BF16, name="spin_in")
@@ -92,25 +86,20 @@ def tile_stsindividuallayer_pb_t_e_kernel(tc, agg, W_words, W_scales, b, out):
         nc.scalar.dma_start(out=b_rows[0:bias_cols, :], in_=b.rearrange("w f (c p) -> (w f c) p", p=P))
         nc.scalar.activation(out=warm[:], in_=warm[:], func=ACT.Sigmoid)
 
-        def load_agg_half(half):
-            pair, h = divmod(half, 2)
+        def load_agg(pair):
             w, i = divmod(pair, BATCH)
             by_partition = agg[i, w].rearrange("(p t) c -> p t c", t=NODE_TILES)
             tiles = HALF_NODES // P
-            nc.sync.dma_start(out=x_raw[half][:], in_=by_partition[:, tiles * h : tiles * (h + 1), :])
-
-        def load_agg(pair):
             for h in range(2):
-                load_agg_half(2 * pair + h)
+                nc.sync.dma_start(out=x_raw[2 * pair + h][:], in_=by_partition[:, tiles * h : tiles * (h + 1), :])
 
-        def load_weights(w, q):
+        def load_weights(w, chunks):
             words = W_words[BRANCHES * w : BRANCHES * (w + 1)].rearrange("f p n t -> p f (n t)").bitcast(I32)
-            for x in range(len(w_codes[w][q]["gate"])):
+            for x in chunks:
                 for part in ("gate", "lin"):
-                    codes = w_codes[w][q][part][x]
-                    width = ROUND_COLS // len(w_codes[w][q][part])
-                    first_col = ROUND_COLS * q + width * x + (CHANNELS if part == "gate" else 0)
-                    nc.sync.dma_start(out=codes[:].bitcast(I32), in_=words[:, :, first_col : first_col + width])
+                    width = CHANNELS // len(w_codes[w][part])
+                    first_col = width * x + (CHANNELS if part == "gate" else 0)
+                    nc.sync.dma_start(out=w_codes[w][part][x][:].bitcast(I32), in_=words[:, :, first_col : first_col + width])
 
         def load_scale_planes(w):
             for quadrant in range(4):
@@ -121,15 +110,14 @@ def tile_stsindividuallayer_pb_t_e_kernel(tc, agg, W_words, W_scales, b, out):
 
         load_agg(0)
         load_scale_planes(0)
-        load_weights(0, 0)
+        load_weights(0, (0, 1))
         load_agg(1)
-        load_weights(0, 1)
+        load_weights(0, (2, 3))
         for w in range(1, WINDOWS):
             load_agg(BATCH * w)
             load_scale_planes(w)
+            load_weights(w, (0, 1))
             load_agg(BATCH * w + 1)
-            for q in range(ROUNDS_PER_PAIR):
-                load_weights(w, q)
 
         def spin(count):
             spun = psum.tile([P, NODES], F32, tag="bank", name="spun")
@@ -176,8 +164,11 @@ def tile_stsindividuallayer_pb_t_e_kernel(tc, agg, W_words, W_scales, b, out):
                     in_=grouped[pair][:, 4 * cols.start : 4 * cols.stop],
                 )
 
-        def halves_of_round(r):
-            return range(HEAD_HALVES if r == 0 else r + AHEAD, min(r + AHEAD, HALVES - 1) + 1)
+        rounds = []
+        for pair in range(PAIRS):
+            for blocks in ((0, 1), (2, 3)) if pair in SHORT_PAIRS else (tuple(range(BLOCKS)),):
+                rounds.append((pair, blocks))
+        halves_of = [[2 * (k + 1), 2 * (k + 1) + 1] if k + 1 < PAIRS else [] for k in range(len(rounds))]
 
         banks = {}
         glus = {}
@@ -185,154 +176,107 @@ def tile_stsindividuallayer_pb_t_e_kernel(tc, agg, W_words, W_scales, b, out):
         merged = {}
         out_flips = {}
 
-        def block_of(r, a):
-            return ROUND_BLOCKS * (r % ROUNDS_PER_PAIR) + a
+        def bias_col(pair, c, f, part):
+            return (BRANCHES * (pair // BATCH) + f) * 2 * BLOCKS + c + (BLOCKS if part == "gate" else 0)
 
-        def bias_col(r, a, f, part):
-            w = (r // ROUNDS_PER_PAIR) // BATCH
-            c = block_of(r, a) + (BLOCKS if part == "gate" else 0)
-            return (BRANCHES * w + f) * 2 * BLOCKS + c
-
-        def node_pieces(r, a):
-            bounds = SPLIT_BLOCKS.get((r, a), (0, NODES))
+        def node_pieces(pair, c):
+            bounds = (0, HALF_NODES, NODES) if (pair, c) == (0, 0) else (0, NODES)
             return [slice(lo, hi) for lo, hi in zip(bounds, bounds[1:])]
 
-        def multiply(r):
-            pair, q = divmod(r, ROUNDS_PER_PAIR)
+        def multiply(pair, c):
             w = pair // BATCH
-            for a in range(ROUND_BLOCKS):
-                for nodes in node_pieces(r, a):
-                    for part in ("gate", "lin"):
-                        for f in range(BRANCHES):
-                            first_col = P * block_of(r, a) + (CHANNELS if part == "gate" else 0)
-                            width = ROUND_COLS // len(w_codes[w][q][part])
-                            x, first_code = divmod(P * a, width)
-                            bank = psum.tile([P, nodes.stop - nodes.start], F32, tag="bank", name="bank")
-                            nc.tensor.matmul_mx(
-                                out=bank[:],
-                                lhsT=w_codes[w][q][part][x][:, f, first_code : first_code + P].bitcast(FP8X4),
-                                lhsT_scale=w_planes[w][4 * f : P, first_col : first_col + P],
-                                rhs=x_codes[pair][:, nodes].bitcast(FP8X4),
-                                rhs_scale=x_scales[pair][:, nodes],
-                                start=True,
-                                stop=True,
-                            )
-                            banks.setdefault((r, a, f, part), []).append((bank, nodes))
+            for nodes in node_pieces(pair, c):
+                for part in ("gate", "lin"):
+                    for f in range(BRANCHES):
+                        first_col = P * c + (CHANNELS if part == "gate" else 0)
+                        width = CHANNELS // len(w_codes[w][part])
+                        x, first_code = divmod(P * c, width)
+                        bank = psum.tile([P, nodes.stop - nodes.start], F32, tag="bank", name="bank")
+                        nc.tensor.matmul_mx(
+                            out=bank[:],
+                            lhsT=w_codes[w][part][x][:, f, first_code : first_code + P].bitcast(FP8X4),
+                            lhsT_scale=w_planes[w][4 * f : P, first_col : first_col + P],
+                            rhs=x_codes[pair][:, nodes].bitcast(FP8X4),
+                            rhs_scale=x_scales[pair][:, nodes],
+                            start=True,
+                            stop=True,
+                        )
+                        banks.setdefault((pair, c, f, part), []).append((bank, nodes))
 
-        def open_gates(r, a):
+        def open_gates(pair, c):
             for f in range(BRANCHES):
-                sigmoids[(r, a, f)] = gates.tile([P, NODES], F32, name="sig")
-            for piece in range(len(node_pieces(r, a))):
+                sigmoids[(pair, c, f)] = gates.tile([P, NODES], F32, name="sig")
+            for piece in range(len(node_pieces(pair, c))):
                 for f in range(BRANCHES):
-                    col = bias_col(r, a, f, "gate")
-                    bank, nodes = banks[(r, a, f, "gate")][piece]
+                    col = bias_col(pair, c, f, "gate")
+                    bank, nodes = banks[(pair, c, f, "gate")][piece]
                     nc.scalar.activation(
-                        out=sigmoids[(r, a, f)][:, nodes],
+                        out=sigmoids[(pair, c, f)][:, nodes],
                         in_=bank[:],
                         func=ACT.Sigmoid,
                         bias=bias[:, col : col + 1],
                         scale=1.0,
                     )
 
-        def gated_branch(r, a, f, piece, part=slice(None)):
-            if (r, a, f) not in glus:
-                glus[(r, a, f)] = branches.tile([P, NODES], F32, name="glu")
-            col = bias_col(r, a, f, "lin")
-            bank, nodes = banks[(r, a, f, "lin")][piece]
+        def gated_branch(pair, c, f, piece, part=slice(None)):
+            if (pair, c, f) not in glus:
+                glus[(pair, c, f)] = branches.tile([P, NODES], F32, name="glu")
+            col = bias_col(pair, c, f, "lin")
+            bank, nodes = banks[(pair, c, f, "lin")][piece]
             nc.vector.scalar_tensor_tensor(
-                out=glus[(r, a, f)][:, nodes][:, part],
+                out=glus[(pair, c, f)][:, nodes][:, part],
                 in0=bank[:, part],
                 scalar=bias[:, col : col + 1],
-                in1=sigmoids[(r, a, f)][:, nodes][:, part],
+                in1=sigmoids[(pair, c, f)][:, nodes][:, part],
                 op0=ALU.add,
                 op1=ALU.mult,
             )
 
-        def gated_branches(r, a):
-            for piece in range(len(node_pieces(r, a))):
+        def gated_branches(pair, c):
+            for piece in range(len(node_pieces(pair, c))):
                 for f in range(BRANCHES):
-                    gated_branch(r, a, f, piece)
+                    gated_branch(pair, c, f, piece)
 
-        def maximum(r, a, out, cols):
-            nc.vector.tensor_tensor(out=out, in0=glus[(r, a, 0)][:, cols], in1=glus[(r, a, 1)][:, cols], op=ALU.max)
+        def maximum(pair, c, out, cols):
+            nc.vector.tensor_tensor(out=out, in0=glus[(pair, c, 0)][:, cols], in1=glus[(pair, c, 1)][:, cols], op=ALU.max)
 
-        def merge(r, a, cols=slice(0, NODES)):
-            if (r, a) not in merged:
-                merged[(r, a)] = [mergeds.tile([P, NODES], F32, name="best")]
-            maximum(r, a, merged[(r, a)][0][:, cols], cols)
+        def merge(pair, c, cols=slice(0, NODES)):
+            if (pair, c) not in merged:
+                merged[(pair, c)] = [mergeds.tile([P, NODES], F32, name="best")]
+            maximum(pair, c, merged[(pair, c)][0][:, cols], cols)
 
-        def gate_and_merge(r, a, pieces):
-            gated_branch(r, a, 0, 0)
+        def gate_and_merge(pair, c, pieces):
+            gated_branch(pair, c, 0, 0)
             width = NODES // pieces
             cols = [slice(width * piece, width * (piece + 1)) for piece in range(pieces)]
-            merged[(r, a)] = []
+            merged[(pair, c)] = []
             for piece in range(pieces + MERGE_LAG):
                 if piece < pieces:
-                    gated_branch(r, a, 1, 0, cols[piece])
+                    gated_branch(pair, c, 1, 0, cols[piece])
                 if piece >= MERGE_LAG:
                     best = mergeds.tile([P, width], F32, name="best")
-                    maximum(r, a, best[:], cols[piece - MERGE_LAG])
-                    merged[(r, a)].append(best)
+                    maximum(pair, c, best[:], cols[piece - MERGE_LAG])
+                    merged[(pair, c)].append(best)
 
-        def half_words(half):
-            pair, h = divmod(half, 2)
-            return grouped[pair][:].bitcast(F32)[:, 2 * HALF_NODES * h : 2 * HALF_NODES * (h + 1)]
+        def transpose_merged(pair, c):
+            tiles = NODE_TILES // len(merged[(pair, c)])
+            out_flips[(pair, c)] = []
+            for best in merged[(pair, c)]:
+                flipped = psum.tile([P, tiles, P], F32, tag="bank", name="out_flip")
+                for t in range(tiles):
+                    nc.tensor.transpose(flipped[:, t, :], best[:, P * t : P * (t + 1)], ident[:])
+                out_flips[(pair, c)].append(flipped)
 
-        pool_parts = (slice(0, POOL_COLS // 2), slice(POOL_COLS // 2, POOL_COLS))
-
-        def pool_start(r):
-            diff = half_words(r + AHEAD)
-            nc.gpsimd.tensor_tensor(
-                out=diff[:, 0:POOL_COLS], in0=glus[(r, 1, 1)][:, 0:POOL_COLS], in1=glus[(r, 1, 0)][:, 0:POOL_COLS], op=ALU.subtract
-            )
-            nc.gpsimd.tensor_scalar(
-                out=diff[:, pool_parts[0]], in0=diff[:, pool_parts[0]], scalar1=0.0, scalar2=None, op0=ALU.max
-            )
-
-        def pool_finish(r):
-            diff = half_words(r + AHEAD)
-            rest = half_words(r + AHEAD + 1)
-            width = POOL_COLS // 2
-            nc.gpsimd.tensor_scalar(out=rest[:, 0:width], in0=diff[:, pool_parts[1]], scalar1=0.0, scalar2=None, op0=ALU.max)
-            for part, gain in zip(pool_parts, (diff[:, pool_parts[0]], rest[:, 0:width])):
-                nc.gpsimd.tensor_tensor(out=merged[(r, 1)][0][:, part], in0=glus[(r, 1, 0)][:, part], in1=gain, op=ALU.add)
-
-        def due(r):
-            blocks = []
-            if r > 0:
-                blocks.append((r - 1, 0))
-                if r - 1 not in POOL_ROUNDS:
-                    blocks.append((r - 1, 1))
-            if r - 1 - POOL_LAG in POOL_ROUNDS:
-                blocks.append((r - 1 - POOL_LAG, 1))
-            return blocks
-
-        def transpose_merged(blocks):
-            for r, a in blocks:
-                tiles = NODE_TILES // len(merged[(r, a)])
-                out_flips[(r, a)] = []
-                for best in merged[(r, a)]:
-                    flipped = psum.tile([P, tiles, P], F32, tag="bank", name="out_flip")
-                    for t in range(tiles):
-                        nc.tensor.transpose(flipped[:, t, :], best[:, P * t : P * (t + 1)], ident[:])
-                    out_flips[(r, a)].append(flipped)
-
-        def store(r, a, copy=None):
-            w, i = divmod(r // ROUNDS_PER_PAIR, BATCH)
+        def store(pair, c, copy):
+            w, i = divmod(pair, BATCH)
             by_partition = out[i, w].rearrange("(p t) c -> p t c", t=NODE_TILES)
-            tiles = NODE_TILES // len(out_flips[(r, a)])
-            first_col = P * block_of(r, a)
-            for piece, flipped in enumerate(out_flips[(r, a)]):
+            tiles = NODE_TILES // len(out_flips[(pair, c)])
+            for piece, flipped in enumerate(out_flips[(pair, c)]):
                 result = results.tile([P, tiles, P], F32, name="result")
-                (copy or nc.scalar.copy)(out=result[:], in_=flipped[:])
+                copy(out=result[:], in_=flipped[:])
                 nc.sync.dma_start(
-                    out=by_partition[:, tiles * piece : tiles * (piece + 1), first_col : first_col + P], in_=result[:]
+                    out=by_partition[:, tiles * piece : tiles * (piece + 1), P * c : P * (c + 1)], in_=result[:]
                 )
-
-        def vector_store(r, pos):
-            for block in due(r)[1:]:
-                if block[0] in VECTOR_SET and pos == VPOS:
-                    store(*block, copy=nc.vector.tensor_copy)
 
         for half in range(2):
             transpose_agg_half(half)
@@ -340,57 +284,69 @@ def tile_stsindividuallayer_pb_t_e_kernel(tc, agg, W_words, W_scales, b, out):
         nc.vector.tensor_copy(out=b_rows_f32[:], in_=b_rows[:])
         b_flip = psum.tile([P, P], F32, tag="bank", name="b_flip")
         nc.tensor.transpose(b_flip[:], b_rows_f32[:], ident[:])
-        for half in range(2, HEAD_HALVES):
-            transpose_agg_half(half)
-            regroup_agg_half(half)
         spin(SPIN_BEFORE_PASSES)
         quantise_agg_half(0)
         nc.vector.tensor_copy(out=bias[:], in_=b_flip[:, 0:bias_cols])
-        for half in range(1, HEAD_HALVES):
-            quantise_agg_half(half)
+        quantise_agg_half(1)
 
-        for r in range(ROUNDS + 1):
-            if r < ROUNDS:
-                multiply(r)
-            if r == ROUNDS:
-                spin(4)
-            transpose_merged(due(r))
-            for half in halves_of_round(r):
+        def half_words(half):
+            pair, h = divmod(half, 2)
+            return grouped[pair][:].bitcast(F32)[:, 2 * HALF_NODES * h : 2 * HALF_NODES * (h + 1)]
+
+        def pool_merge(pair, c, half):
+            diff = half_words(half)[:, 0:POOL_COLS]
+            cols = slice(0, POOL_COLS)
+            nc.gpsimd.tensor_tensor(out=diff, in0=glus[(pair, c, 1)][:, cols], in1=glus[(pair, c, 0)][:, cols], op=ALU.subtract)
+            nc.gpsimd.tensor_scalar(out=diff, in0=diff, scalar1=0.0, scalar2=None, op0=ALU.max)
+            nc.gpsimd.tensor_tensor(out=merged[(pair, c)][0][:, cols], in0=glus[(pair, c, 0)][:, cols], in1=diff, op=ALU.add)
+
+        def pool_block(k):
+            if 0 <= k < len(rounds) and rounds[k][0] in POOL_PAIRS:
+                return [(rounds[k][0], rounds[k][1][-1])]
+            return []
+
+        last = len(rounds) - 1
+        for k in range(len(rounds) + 1):
+            pair, blocks = rounds[k] if k <= last else (None, ())
+            due = [(rounds[k - 1][0], c) for c in rounds[k - 1][1]] if k > 0 else []
+            due = [block for block in due if block not in pool_block(k - 1)] + pool_block(k - 2)
+            halves = halves_of[k] if k <= last else []
+            for c in blocks:
+                multiply(pair, c)
+            if k > last:
+                spin(SPIN_TAIL)
+            for block in due:
+                transpose_merged(*block)
+            for half in halves:
                 transpose_agg_half(half)
-            if r < ROUNDS:
-                open_gates(r, 0)
-                open_gates(r, 1)
-            if r > 0:
-                store(r - 1, 0)
-            if r > 0:
-                for half in halves_of_round(r - 1):
-                    quantise_agg_half(half)
-            if r < ROUNDS - 1:
-                gated_branches(r, 0)
-            elif r == ROUNDS - 1:
-                gate_and_merge(r, 0, LAST_PIECES[0])
-            if r == 0:
-                merge(r, 0, slice(0, HALF_NODES))
-            for block in due(r)[1:]:
-                if block[0] not in VECTOR_SET:
-                    store(*block)
-            vector_store(r, 0)
-            if r - 1 in POOL_ROUNDS:
-                pool_start(r - 1)
-            if r - 2 in POOL_ROUNDS:
-                pool_finish(r - 2)
-            for half in halves_of_round(r):
+            for c in blocks:
+                open_gates(pair, c)
+            by_vector = due[-1:] if k in VECTOR_SET else []
+            for block in due:
+                if block not in by_vector:
+                    store(*block, nc.scalar.copy)
+            for half in halves:
                 regroup_agg_half(half)
-            if r < ROUNDS - 1:
-                if r == 0:
-                    gated_branches(r, 1)
-                else:
-                    gated_branch(r, 1, 0, 0)
-                    vector_store(r, 1)
-                    gated_branch(r, 1, 1, 0)
-                    vector_store(r, 2)
-                merge(r, 0, slice(HALF_NODES if r == 0 else 0, NODES))
-                merge(r, 1, slice(POOL_COLS if r in POOL_ROUNDS else 0, NODES))
-                vector_store(r, 3)
-            elif r == ROUNDS - 1:
-                gate_and_merge(r, 1, LAST_PIECES[1])
+            if k > 0:
+                for half in halves_of[k - 1]:
+                    quantise_agg_half(half)
+                for block in pool_block(k - 1):
+                    pool_merge(*block, halves_of[k - 1][-1])
+            if k == last:
+                for c, pieces in zip(blocks, LAST_PIECES):
+                    gate_and_merge(pair, c, pieces)
+            else:
+                late = LATE_MERGE and len(blocks) > 2
+                for j, c in enumerate(blocks):
+                    gated_branches(pair, c)
+                    if j > 0 and not late:
+                        merge(pair, blocks[j - 1], slice(HALF_NODES if (pair, j) == (0, 1) and k == 0 else 0, NODES))
+                    elif k == 0:
+                        merge(pair, c, slice(0, HALF_NODES))
+                    if j == len(blocks) - 1:
+                        for block in by_vector:
+                            store(*block, nc.vector.tensor_copy)
+                        if late:
+                            for a in blocks[:-1]:
+                                merge(pair, a)
+                        merge(pair, c, slice(POOL_COLS if (pair, c) in pool_block(k) else 0, NODES))

from contextlib import ExitStack

import concourse.mybir as mybir
from concourse.masks import make_identity

F32 = mybir.dt.float32
BF16 = mybir.dt.bfloat16
I32 = mybir.dt.int32
U32 = mybir.dt.uint32
U8 = mybir.dt.uint8
FP8X4 = mybir.dt.float8_e4m3fn_x4
ALU = mybir.AluOpType
ACT = mybir.ActivationFunctionType

P = 128
BATCH = 2
WINDOWS = 4
BRANCHES = 2
NODES = 512
CHANNELS = 512
PAIRS = WINDOWS * BATCH
NODE_TILES = NODES // P
BLOCKS = CHANNELS // P
HALF_NODES = NODES // 2
HALVES = PAIRS * 2
SHORT_PAIRS = (0, 6, 7)
VECTOR_SET = (4, 5, 6)
POOL_PAIRS = (1, 2, 3, 4)
POOL_COLS = 448
LATE_MERGE = 1
SPIN_HEAD = 4
SPIN_BEFORE_PASSES = 1
SPIN_TAIL = 4
FINE_HALVES = 2
LAST_PIECES = (2, 4)
MERGE_LAG = 1
GATES = 10
BRANCH_BUFS = 12
MERGED = 8
RESULTS = 8

FLOPS = 2 * BATCH * WINDOWS * BRANCHES * NODES * CHANNELS * 2 * CHANNELS


def tile_stsindividuallayer_pb_t_e_kernel(tc, agg, W_words, W_scales, b, out):
    nc = tc.nc
    with ExitStack() as ctx:
        ctx.enter_context(tc.manual_schedule())
        keep = ctx.enter_context(tc.tile_pool(name="keep", bufs=1))
        gates = ctx.enter_context(tc.tile_pool(name="gates", bufs=GATES))
        branches = ctx.enter_context(tc.tile_pool(name="branches", bufs=BRANCH_BUFS))
        mergeds = ctx.enter_context(tc.tile_pool(name="mergeds", bufs=MERGED))
        results = ctx.enter_context(tc.tile_pool(name="results", bufs=RESULTS))
        psum = ctx.enter_context(tc.psum_pool(name="psum", bufs=8))

        x_raw = [keep.tile([P, HALF_NODES // P, CHANNELS], BF16, name="x_raw%d" % half) for half in range(HALVES)]
        grouped = [keep.tile([P, NODES * 4], BF16, name="grouped%d" % pair, align_bytes=256) for pair in range(PAIRS)]
        x_codes = [keep.tile([P, NODES], U32, name="x_codes%d" % pair, align_bytes=256) for pair in range(PAIRS)]
        x_scales = [keep.tile([P, NODES], U8, name="x_scales%d" % pair, align_bytes=256) for pair in range(PAIRS)]
        w_codes = [
            {
                part: [
                    keep.tile([P, BRANCHES, width], U32, name="w_%s%d_%d" % (part, w, x), align_bytes=256)
                    for x in range(CHANNELS // width)
                ]
                for part in ("lin", "gate")
            }
            for w in range(WINDOWS)
            for width in (P if w == 0 else 2 * P,)
        ]
        w_planes = [keep.tile([P, 2 * CHANNELS], U8, name="w_planes%d" % w, align_bytes=256) for w in range(WINDOWS)]
        ident = keep.tile([P, P], F32, name="ident")
        b_rows = keep.tile([P, P], BF16, name="b_rows")
        b_rows_f32 = keep.tile([P, P], F32, name="b_rows_f32")
        bias_cols = WINDOWS * BRANCHES * 2 * BLOCKS
        bias = keep.tile([P, bias_cols], F32, name="bias")
        warm = keep.tile([P, 1], F32, name="warm")
        spin_in = keep.tile([P, NODES], BF16, name="spin_in")

        for plane_tile in w_planes:
            nc.vector.memset(plane_tile[:].bitcast(I32), 0)
        nc.vector.memset(b_rows[bias_cols:P, :], 0.0)
        nc.gpsimd.memset(warm[:], 0.0)
        nc.gpsimd.memset(spin_in[:], 0.0)
        make_identity(nc, ident[:])
        nc.scalar.dma_start(out=b_rows[0:bias_cols, :], in_=b.rearrange("w f (c p) -> (w f c) p", p=P))
        nc.scalar.activation(out=warm[:], in_=warm[:], func=ACT.Sigmoid)

        def load_agg(pair):
            w, i = divmod(pair, BATCH)
            by_partition = agg[i, w].rearrange("(p t) c -> p t c", t=NODE_TILES)
            tiles = HALF_NODES // P
            for h in range(2):
                nc.sync.dma_start(out=x_raw[2 * pair + h][:], in_=by_partition[:, tiles * h : tiles * (h + 1), :])

        def load_weights(w, chunks):
            words = W_words[BRANCHES * w : BRANCHES * (w + 1)].rearrange("f p n t -> p f (n t)").bitcast(I32)
            for x in chunks:
                for part in ("gate", "lin"):
                    width = CHANNELS // len(w_codes[w][part])
                    first_col = width * x + (CHANNELS if part == "gate" else 0)
                    nc.sync.dma_start(out=w_codes[w][part][x][:].bitcast(I32), in_=words[:, :, first_col : first_col + width])

        def load_scale_planes(w):
            for quadrant in range(4):
                nc.sync.dma_start(
                    out=w_planes[w][32 * quadrant : 32 * quadrant + 4 * BRANCHES, :].bitcast(I32),
                    in_=W_scales[BRANCHES * w : BRANCHES * (w + 1), 4 * quadrant : 4 * quadrant + 4, :].bitcast(I32),
                )

        load_agg(0)
        load_scale_planes(0)
        load_weights(0, (0, 1))
        load_agg(1)
        load_weights(0, (2, 3))
        for w in range(1, WINDOWS):
            load_agg(BATCH * w)
            load_scale_planes(w)
            load_weights(w, (0, 1))
            load_agg(BATCH * w + 1)

        def spin(count):
            spun = psum.tile([P, NODES], F32, tag="bank", name="spun")
            for i in range(count):
                nc.tensor.matmul(spun[:], lhsT=spin_in[:, 0:P], rhs=spin_in[:], start=True, stop=True)

        spin(SPIN_HEAD)

        agg_flips = {}

        def transpose_agg_half(half):
            tiles = HALF_NODES // P
            per_bank = 1 if half < FINE_HALVES else tiles
            agg_flips[half] = []
            for first in range(0, tiles, per_bank):
                flipped = psum.tile([P, 2, P * per_bank], F32, tag="bank", name="agg_flip")
                for a in range(per_bank):
                    words = x_raw[half][:, first + a, :].bitcast(F32)
                    for u in range(2):
                        nc.tensor.transpose(flipped[:, u, P * a : P * (a + 1)], words[:, u : CHANNELS // 2 : 2], ident[:])
                agg_flips[half].append(flipped)

        def agg_pieces(half):
            pair, h = divmod(half, 2)
            width = HALF_NODES // len(agg_flips[half])
            first = HALF_NODES * h
            return pair, [slice(c, c + width) for c in range(first, first + HALF_NODES, width)]

        def regroup_agg_half(half):
            pair, pieces = agg_pieces(half)
            for flipped, cols in zip(agg_flips[half], pieces):
                words = grouped[pair][:].bitcast(F32)[:, 2 * cols.start : 2 * cols.stop]
                nc.scalar.copy(
                    out=words.rearrange("p (c u) -> p c u", u=2),
                    in_=flipped[:].rearrange("p u c -> p c u"),
                )

        def quantise_agg_half(half):
            pair, pieces = agg_pieces(half)
            for cols in pieces:
                nc.vector.quantize_mx(
                    out=x_codes[pair][:, cols].bitcast(FP8X4),
                    scales=x_scales[pair][:, cols],
                    in_=grouped[pair][:, 4 * cols.start : 4 * cols.stop],
                )

        rounds = []
        for pair in range(PAIRS):
            for blocks in ((0, 1), (2, 3)) if pair in SHORT_PAIRS else (tuple(range(BLOCKS)),):
                rounds.append((pair, blocks))
        halves_of = [[2 * (k + 1), 2 * (k + 1) + 1] if k + 1 < PAIRS else [] for k in range(len(rounds))]

        banks = {}
        glus = {}
        sigmoids = {}
        merged = {}
        out_flips = {}

        def bias_col(pair, c, f, part):
            return (BRANCHES * (pair // BATCH) + f) * 2 * BLOCKS + c + (BLOCKS if part == "gate" else 0)

        def node_pieces(pair, c):
            bounds = (0, HALF_NODES, NODES) if (pair, c) == (0, 0) else (0, NODES)
            return [slice(lo, hi) for lo, hi in zip(bounds, bounds[1:])]

        def multiply(pair, c):
            w = pair // BATCH
            for nodes in node_pieces(pair, c):
                for part in ("gate", "lin"):
                    for f in range(BRANCHES):
                        first_col = P * c + (CHANNELS if part == "gate" else 0)
                        width = CHANNELS // len(w_codes[w][part])
                        x, first_code = divmod(P * c, width)
                        bank = psum.tile([P, nodes.stop - nodes.start], F32, tag="bank", name="bank")
                        nc.tensor.matmul_mx(
                            out=bank[:],
                            lhsT=w_codes[w][part][x][:, f, first_code : first_code + P].bitcast(FP8X4),
                            lhsT_scale=w_planes[w][4 * f : P, first_col : first_col + P],
                            rhs=x_codes[pair][:, nodes].bitcast(FP8X4),
                            rhs_scale=x_scales[pair][:, nodes],
                            start=True,
                            stop=True,
                        )
                        banks.setdefault((pair, c, f, part), []).append((bank, nodes))

        def open_gates(pair, c):
            for f in range(BRANCHES):
                sigmoids[(pair, c, f)] = gates.tile([P, NODES], F32, name="sig")
            for piece in range(len(node_pieces(pair, c))):
                for f in range(BRANCHES):
                    col = bias_col(pair, c, f, "gate")
                    bank, nodes = banks[(pair, c, f, "gate")][piece]
                    nc.scalar.activation(
                        out=sigmoids[(pair, c, f)][:, nodes],
                        in_=bank[:],
                        func=ACT.Sigmoid,
                        bias=bias[:, col : col + 1],
                        scale=1.0,
                    )

        def gated_branch(pair, c, f, piece, part=slice(None)):
            if (pair, c, f) not in glus:
                glus[(pair, c, f)] = branches.tile([P, NODES], F32, name="glu")
            col = bias_col(pair, c, f, "lin")
            bank, nodes = banks[(pair, c, f, "lin")][piece]
            nc.vector.scalar_tensor_tensor(
                out=glus[(pair, c, f)][:, nodes][:, part],
                in0=bank[:, part],
                scalar=bias[:, col : col + 1],
                in1=sigmoids[(pair, c, f)][:, nodes][:, part],
                op0=ALU.add,
                op1=ALU.mult,
            )

        def gated_branches(pair, c):
            for piece in range(len(node_pieces(pair, c))):
                for f in range(BRANCHES):
                    gated_branch(pair, c, f, piece)

        def maximum(pair, c, out, cols):
            nc.vector.tensor_tensor(out=out, in0=glus[(pair, c, 0)][:, cols], in1=glus[(pair, c, 1)][:, cols], op=ALU.max)

        def merge(pair, c, cols=slice(0, NODES)):
            if (pair, c) not in merged:
                merged[(pair, c)] = [mergeds.tile([P, NODES], F32, name="best")]
            maximum(pair, c, merged[(pair, c)][0][:, cols], cols)

        def gate_and_merge(pair, c, pieces):
            gated_branch(pair, c, 0, 0)
            width = NODES // pieces
            cols = [slice(width * piece, width * (piece + 1)) for piece in range(pieces)]
            merged[(pair, c)] = []
            for piece in range(pieces + MERGE_LAG):
                if piece < pieces:
                    gated_branch(pair, c, 1, 0, cols[piece])
                if piece >= MERGE_LAG:
                    best = mergeds.tile([P, width], F32, name="best")
                    maximum(pair, c, best[:], cols[piece - MERGE_LAG])
                    merged[(pair, c)].append(best)

        def transpose_merged(pair, c):
            tiles = NODE_TILES // len(merged[(pair, c)])
            out_flips[(pair, c)] = []
            for best in merged[(pair, c)]:
                flipped = psum.tile([P, tiles, P], F32, tag="bank", name="out_flip")
                for t in range(tiles):
                    nc.tensor.transpose(flipped[:, t, :], best[:, P * t : P * (t + 1)], ident[:])
                out_flips[(pair, c)].append(flipped)

        def store(pair, c, copy):
            w, i = divmod(pair, BATCH)
            by_partition = out[i, w].rearrange("(p t) c -> p t c", t=NODE_TILES)
            tiles = NODE_TILES // len(out_flips[(pair, c)])
            for piece, flipped in enumerate(out_flips[(pair, c)]):
                result = results.tile([P, tiles, P], F32, name="result")
                copy(out=result[:], in_=flipped[:])
                nc.sync.dma_start(
                    out=by_partition[:, tiles * piece : tiles * (piece + 1), P * c : P * (c + 1)], in_=result[:]
                )

        for half in range(2):
            transpose_agg_half(half)
            regroup_agg_half(half)
        nc.vector.tensor_copy(out=b_rows_f32[:], in_=b_rows[:])
        b_flip = psum.tile([P, P], F32, tag="bank", name="b_flip")
        nc.tensor.transpose(b_flip[:], b_rows_f32[:], ident[:])
        spin(SPIN_BEFORE_PASSES)
        quantise_agg_half(0)
        nc.vector.tensor_copy(out=bias[:], in_=b_flip[:, 0:bias_cols])
        quantise_agg_half(1)

        def half_words(half):
            pair, h = divmod(half, 2)
            return grouped[pair][:].bitcast(F32)[:, 2 * HALF_NODES * h : 2 * HALF_NODES * (h + 1)]

        def pool_merge(pair, c, half):
            diff = half_words(half)[:, 0:POOL_COLS]
            cols = slice(0, POOL_COLS)
            nc.gpsimd.tensor_tensor(out=diff, in0=glus[(pair, c, 1)][:, cols], in1=glus[(pair, c, 0)][:, cols], op=ALU.subtract)
            nc.gpsimd.tensor_scalar(out=diff, in0=diff, scalar1=0.0, scalar2=None, op0=ALU.max)
            nc.gpsimd.tensor_tensor(out=merged[(pair, c)][0][:, cols], in0=glus[(pair, c, 0)][:, cols], in1=diff, op=ALU.add)

        def pool_block(k):
            if 0 <= k < len(rounds) and rounds[k][0] in POOL_PAIRS:
                return [(rounds[k][0], rounds[k][1][-1])]
            return []

        last = len(rounds) - 1
        for k in range(len(rounds) + 1):
            pair, blocks = rounds[k] if k <= last else (None, ())
            due = [(rounds[k - 1][0], c) for c in rounds[k - 1][1]] if k > 0 else []
            due = [block for block in due if block not in pool_block(k - 1)] + pool_block(k - 2)
            halves = halves_of[k] if k <= last else []
            for c in blocks:
                multiply(pair, c)
            if k > last:
                spin(SPIN_TAIL)
            for block in due:
                transpose_merged(*block)
            for half in halves:
                transpose_agg_half(half)
            for c in blocks:
                open_gates(pair, c)
            by_vector = due[-1:] if k in VECTOR_SET else []
            for block in due:
                if block not in by_vector:
                    store(*block, nc.scalar.copy)
            for half in halves:
                regroup_agg_half(half)
            if k > 0:
                for half in halves_of[k - 1]:
                    quantise_agg_half(half)
                for block in pool_block(k - 1):
                    pool_merge(*block, halves_of[k - 1][-1])
            if k == last:
                for c, pieces in zip(blocks, LAST_PIECES):
                    gate_and_merge(pair, c, pieces)
            else:
                late = LATE_MERGE and len(blocks) > 2
                for j, c in enumerate(blocks):
                    gated_branches(pair, c)
                    if j > 0 and not late:
                        merge(pair, blocks[j - 1], slice(HALF_NODES if (pair, j) == (0, 1) and k == 0 else 0, NODES))
                    elif k == 0:
                        merge(pair, c, slice(0, HALF_NODES))
                    if j == len(blocks) - 1:
                        for block in by_vector:
                            store(*block, nc.vector.tensor_copy)
                        if late:
                            for a in blocks[:-1]:
                                merge(pair, a)
                        merge(pair, c, slice(POOL_COLS if (pair, c) in pool_block(k) else 0, NODES))
